import numpy as np
import ml_dtypes


def mxq(x, axis, fmt="e4m3"):
    dtype, down = {"e4m3": (ml_dtypes.float8_e4m3fn, 7), "e5m2": (ml_dtypes.float8_e5m2, 14)}[fmt]
    v = np.moveaxis(np.asarray(x, np.float32).astype(ml_dtypes.bfloat16).astype(np.float64), axis, -1)
    blocks = v.reshape(v.shape[:-1] + (-1, 32))
    amax = np.abs(blocks).max(-1, keepdims=True)
    byte = np.maximum(np.where(amax > 0, np.frexp(amax)[1] - 1 + 127, 0) - down, 1)
    scale = np.exp2(byte - 127.0)
    codes = (blocks / scale).astype(np.float32).astype(dtype).astype(np.float64)
    return np.moveaxis((codes * scale).reshape(v.shape), -1, axis)


WIDE = False


def mx_kscale(k):
    if not WIDE:
        return np.ones(k)
    levels = np.array([10, -10, 5, -5, 0])
    if k % 512:
        return np.exp2(np.random.permutation(np.resize(levels, k // 32))).repeat(32)
    a = np.empty((k // 512, 16))
    for p in range(k // 512):
        a[p, :8] = np.random.permutation(np.resize(levels, 8))
        for g in range(8):
            far = levels[np.abs(levels - a[p, g]) >= 10]
            a[p, g + 8] = far[np.random.randint(len(far))]
    return np.exp2(a.ravel()).repeat(32)


BF16 = ml_dtypes.bfloat16


def bf(x):
    return np.asarray(x, np.float32).astype(BF16)


def f64(x):
    return np.asarray(x).astype(np.float64)


B, R, RS, RED, F1, F2, NC = 8192, 64, 60, 16, 128, 512, 256
C = R * RED
EPS = 1e-5
SLOPE = 0.3


def bn_train(h, gamma, beta):
    mean = h.mean(axis=0)
    var = h.var(axis=0)
    return (h - mean) * (1.0 / np.sqrt(var + EPS)) * gamma + beta


def setup_inputs():
    s = mx_kscale(C)
    sr = s.reshape(R, RED)
    sig = np.exp2(np.random.uniform(-8.0, 1.0, (R, RED)))
    off = 0.7 * np.random.standard_normal((R, RED))
    return {"h_enc": bf((np.random.standard_normal((B, R, RED)) + off) * sig),
            "enc_gamma": bf((1.0 + 0.1 * np.random.standard_normal((R, RED))) * sr),
            "enc_beta": bf(0.3 * np.random.standard_normal((R, RED)) * sr),
            "w1": bf(np.random.standard_normal((F1, C)) / np.sqrt(C) / s[None, :]),
            "b1": bf(0.3 * np.random.standard_normal(F1))}


def reference(h_enc, enc_gamma, enc_beta, w1, b1):
    h = bn_train(f64(h_enc), f64(enc_gamma), f64(enc_beta))
    h = np.where(h >= 0, h, SLOPE * h)
    c = h.reshape(B, C)
    return (mxq(c, 1, "e4m3") @ mxq(f64(w1), 1, "e4m3").T) + f64(b1)

@@ -1,0 +1,282 @@
+from contextlib import ExitStack
+
+import concourse.mybir as mybir
+from concourse.masks import make_identity
+
+F32 = mybir.dt.float32
+BF16 = mybir.dt.bfloat16
+U32 = mybir.dt.uint32
+U8 = mybir.dt.uint8
+FP8X4 = mybir.dt.float8_e4m3fn_x4
+ALU = mybir.AluOpType
+ACT = mybir.ActivationFunctionType
+AXIS_X = mybir.AxisListType.X
+
+P = 128
+BATCH = 8192
+CHANNELS = 1024
+FEATURES = 128
+EPS = 1e-5
+SLOPE = 0.3
+
+ROW_TILES = 4
+CHUNK = P * ROW_TILES
+CHUNKS = BATCH // CHUNK
+WORDS = CHANNELS // 2
+SLABS = WORDS // P
+PASSES = 2
+BN_WIDTH = 512
+BN_CALLS = 2 * CHUNK // BN_WIDTH
+BN_SLOTS = CHUNKS * BN_CALLS
+
+FLOPS = 2 * BATCH * CHANNELS * FEATURES
+
+
+def scalar_takes(c, s):
+    return s == 3 or (s == 2 and c % 2 == 0)
+
+
+def transpose_slab(nc, bank, x_chunk, slab, ident):
+    first = 256 * (slab // 2) + slab % 2
+    for j in range(ROW_TILES):
+        nc.tensor.transpose(
+            out=bank[:, j * P : (j + 1) * P],
+            in_=x_chunk[:, j, :].bitcast(F32)[:, first : first + 2 * P - 1 : 2],
+            identity=ident[:],
+        )
+
+
+def half(bank, e):
+    return bank[:].bitcast(BF16).rearrange("p (b e) -> p b e", e=2)[:, :, e]
+
+
+def tile_roibaseline_pa_t_kernel(tc, h_enc, enc_gamma, enc_beta, w1, b1, out):
+    nc = tc.nc
+    with ExitStack() as ctx:
+        keep = ctx.enter_context(tc.tile_pool(name="keep", bufs=1))
+        junk_pool = ctx.enter_context(tc.tile_pool(name="junk", bufs=4))
+        y_pool = ctx.enter_context(tc.tile_pool(name="y", bufs=3))
+        c_pool = ctx.enter_context(tc.tile_pool(name="c", bufs=3))
+        q_pool = ctx.enter_context(tc.tile_pool(name="q", bufs=3))
+        o_pool = ctx.enter_context(tc.tile_pool(name="o", bufs=3))
+        xt_psum = ctx.enter_context(tc.psum_pool(name="xt", bufs=4))
+        acc_psum = ctx.enter_context(tc.psum_pool(name="acc", bufs=2))
+        back_psum = ctx.enter_context(tc.psum_pool(name="back", bufs=1))
+        sum_psum = ctx.enter_context(tc.psum_pool(name="sum", bufs=1))
+
+        ident = keep.tile([P, P], F32, name="ident")
+        make_identity(nc, ident[:])
+        ones = keep.tile([P, 1], BF16, name="ones")
+        nc.vector.memset(ones[:], 1.0)
+        minus_half = keep.tile([P, 4], F32, name="minus_half")
+        nc.vector.memset(minus_half[:], -0.5)
+
+        w_rows = keep.tile([P, CHANNELS], BF16, name="w_rows")
+        nc.scalar.dma_start(out=w_rows[:], in_=w1)
+        x_chunks = []
+        for c in range(CHUNKS):
+            x_chunk = keep.tile([P, ROW_TILES, CHANNELS], BF16, name="x%d" % c)
+            nc.sync.dma_start(
+                out=x_chunk[:],
+                in_=h_enc[c * CHUNK : (c + 1) * CHUNK].rearrange(
+                    "(p j) r o -> p j (r o)", j=ROW_TILES
+                ),
+            )
+            x_chunks.append(x_chunk)
+        gamma_bf = keep.tile([P, PASSES, 4], BF16, name="gamma_bf")
+        beta_bf = keep.tile([P, PASSES, 4], BF16, name="beta_bf")
+        bias_bf = keep.tile([P, 1], BF16, name="bias_bf")
+        nc.sync.dma_start(
+            out=gamma_bf[:],
+            in_=enc_gamma.rearrange("r o -> (r o)").rearrange("(g p t) -> p g t", g=PASSES, p=P),
+        )
+        nc.sync.dma_start(
+            out=beta_bf[:],
+            in_=enc_beta.rearrange("r o -> (r o)").rearrange("(g p t) -> p g t", g=PASSES, p=P),
+        )
+        nc.sync.dma_start(out=bias_bf[:], in_=b1.rearrange("(f o) -> f o", o=1))
+
+        w_bank = xt_psum.tile([P, SLABS * P], F32, tag="xt", name="w_bank")
+        for s in range(SLABS):
+            first = 256 * (s // 2) + s % 2
+            nc.tensor.transpose(
+                out=w_bank[:, s * P : (s + 1) * P],
+                in_=w_rows[:].bitcast(F32)[:, first : first + 2 * P - 1 : 2],
+                identity=ident[:],
+            )
+        w_grouped = keep.tile([P, PASSES * FEATURES * 4], BF16, name="w_grouped", align_bytes=64)
+        nc.vector.tensor_copy(
+            out=w_grouped[:].bitcast(F32).rearrange("p (g f u) -> p g f u", g=PASSES, u=2),
+            in_=w_bank[:].rearrange("p (g u f) -> p g f u", g=PASSES, u=2),
+        )
+        w_codes = keep.tile([P, PASSES * FEATURES], U32, name="w_codes", align_bytes=64)
+        w_scales = keep.tile([P, PASSES * FEATURES], U8, name="w_scales", align_bytes=64)
+        nc.vector.quantize_mx(out=w_codes[:].bitcast(FP8X4), scales=w_scales[:], in_=w_grouped[:])
+
+        bn_parts = keep.tile([P, SLABS, 1 + BN_SLOTS, 6], F32, name="bn_parts")
+        neg_x0 = keep.tile([P, 2, 2], F32, name="neg_x0")
+        sq_parts = keep.tile([P, 2, 2, CHUNKS], F32, name="sq_parts")
+        sum_parts = sum_psum.tile([P, 2, 2, CHUNKS], F32, name="sum_parts")
+        bn_used = [1, 1, 1, 1]
+        for c in range(CHUNKS):
+            for s in range(SLABS):
+                bank = xt_psum.tile([P, CHUNK], F32, tag="xt", name="bank_a")
+                transpose_slab(nc, bank, x_chunks[c], s, ident)
+                if not scalar_takes(c, s):
+                    for h in range(BN_CALLS):
+                        nc.vector.bn_stats(
+                            out=bn_parts[:, s, bn_used[s], :],
+                            in_=bank[:].bitcast(BF16)[:, h * BN_WIDTH : (h + 1) * BN_WIDTH],
+                        )
+                        bn_used[s] += 1
+                    continue
+                u = s - 2
+                if c == 0:
+                    nc.scalar.mul(
+                        out=neg_x0[:, u, :], in_=bank[:].bitcast(BF16)[:, 0:2], mul=-1.0
+                    )
+                for e in range(2):
+                    junk = junk_pool.tile([P, CHUNK], BF16, name="junk")
+                    nc.scalar.activation(
+                        out=junk[:],
+                        in_=half(bank, e),
+                        func=ACT.Square,
+                        bias=neg_x0[:, u, e : e + 1],
+                        scale=1.0,
+                        accum_out=sq_parts[:, u, e, c : c + 1],
+                    )
+                    first = 512 + 2 * u + e
+                    for j in range(ROW_TILES):
+                        nc.tensor.matmul(
+                            out=sum_parts[:, u, e, c : c + 1],
+                            lhsT=x_chunks[c][:, j, first : first + 4 * P - 3 : 4],
+                            rhs=ones[:],
+                            start=(j == 0),
+                            stop=(j == ROW_TILES - 1),
+                        )
+
+        gamma = keep.tile([P, SLABS * 2], F32, name="gamma")
+        beta = keep.tile([P, SLABS * 2], F32, name="beta")
+        bias = keep.tile([P, 1], F32, name="bias")
+        nc.vector.tensor_copy(out=gamma[:], in_=gamma_bf[:].rearrange("p g t -> p (g t)"))
+        nc.vector.tensor_copy(out=beta[:], in_=beta_bf[:].rearrange("p g t -> p (g t)"))
+        nc.vector.tensor_copy(out=bias[:], in_=bias_bf[:])
+
+        def scale_and_shift(g):
+            mean_var = keep.tile([P, 4, 2], F32, name="mean_var%d" % g)
+            for t in range(4):
+                s = 2 * g + t // 2
+                e = t % 2
+                first_slot = 0 if s >= 2 else 1
+                nc.vector.bn_aggr(
+                    out=mean_var[:, t, :],
+                    in_=bn_parts[:, s, first_slot : bn_used[s], 3 * e : 3 * e + 3],
+                )
+            scale = keep.tile([P, 4], F32, name="scale%d" % g)
+            shift = keep.tile([P, 4], F32, name="shift%d" % g)
+            nc.vector.tensor_scalar_add(out=scale[:], in0=mean_var[:, :, 1], scalar1=EPS)
+            nc.gpsimd.tensor_tensor(out=scale[:], in0=scale[:], in1=minus_half[:], op=ALU.pow)
+            nc.vector.tensor_mul(out=scale[:], in0=scale[:], in1=gamma[:, 4 * g : 4 * g + 4])
+            nc.vector.tensor_mul(out=shift[:], in0=mean_var[:, :, 0], in1=scale[:])
+            nc.vector.tensor_sub(out=shift[:], in0=beta[:, 4 * g : 4 * g + 4], in1=shift[:])
+            return scale, shift
+
+        affine = [scale_and_shift(0)]
+
+        x_sum = keep.tile([P, 2, 2], F32, name="x_sum")
+        sq_sum = keep.tile([P, 2, 2], F32, name="sq_sum")
+        off = keep.tile([P, 2, 2], F32, name="off")
+        for u in range(2):
+            step = 2 - u
+            rows = float(BATCH // step)
+            share = bn_parts[:, 2 + u, 0, :].rearrange("p (e k) -> p e k", k=3)
+            nc.vector.memset(share[:, :, 0], rows)
+            nc.vector.tensor_reduce(
+                out=x_sum[:, u, :], in_=sum_parts[:, u, :, 0:CHUNKS:step], axis=AXIS_X, op=ALU.add
+            )
+            nc.vector.tensor_reduce(
+                out=sq_sum[:, u, :], in_=sq_parts[:, u, :, 0:CHUNKS:step], axis=AXIS_X, op=ALU.add
+            )
+            nc.vector.tensor_scalar_mul(out=share[:, :, 1], in0=x_sum[:, u, :], scalar1=1.0 / rows)
+            nc.vector.tensor_add(out=off[:, u, :], in0=share[:, :, 1], in1=neg_x0[:, u, :])
+            nc.vector.tensor_mul(out=off[:, u, :], in0=off[:, u, :], in1=off[:, u, :])
+            nc.vector.scalar_tensor_tensor(
+                out=share[:, :, 2],
+                in0=off[:, u, :],
+                scalar=-rows,
+                in1=sq_sum[:, u, :],
+                op0=ALU.mult,
+                op1=ALU.add,
+            )
+
+        affine.append(scale_and_shift(1))
+
+        for c in range(CHUNKS):
+            codes = q_pool.tile([P, PASSES, CHUNK], U32, name="codes", align_bytes=64)
+            scales = q_pool.tile([P, PASSES, CHUNK], U8, name="scales", align_bytes=64)
+            for g in range(PASSES):
+                y = y_pool.tile([P, 4, CHUNK], F32, name="y")
+                for u in range(2):
+                    bank = xt_psum.tile([P, CHUNK], F32, tag="xt", name="bank_b")
+                    transpose_slab(nc, bank, x_chunks[c], 2 * g + u, ident)
+                    for e in range(2):
+                        t = 2 * u + e
+                        nc.scalar.activation(
+                            out=y[:, t, :],
+                            in_=half(bank, e),
+                            func=ACT.Identity,
+                            bias=affine[g][1][:, t : t + 1],
+                            scale=affine[g][0][:, t : t + 1],
+                        )
+                pairs = c_pool.tile([P, 2, CHUNK, 2], BF16, name="pairs")
+                for u in range(2):
+                    y_by_row = y[:, 2 * u : 2 * u + 2, :].rearrange("p e b -> p b e")
+                    nc.vector.scalar_tensor_tensor(
+                        out=pairs[:, u, :, :],
+                        in0=y_by_row,
+                        scalar=SLOPE,
+                        in1=y_by_row,
+                        op0=ALU.mult,
+                        op1=ALU.max,
+                    )
+                grouped = c_pool.tile([P, CHUNK, 4], BF16, name="grouped", align_bytes=64)
+                nc.vector.tensor_copy(
+                    out=grouped[:].rearrange("p b t -> p (b t)").bitcast(F32).rearrange(
+                        "p (b u) -> p b u", u=2
+                    ),
+                    in_=pairs[:].rearrange("p u b e -> p (u b e)").bitcast(F32).rearrange(
+                        "p (u b) -> p b u", u=2
+                    ),
+                )
+                nc.vector.quantize_mx(
+                    out=codes[:, g, :].bitcast(FP8X4),
+                    scales=scales[:, g, :],
+                    in_=grouped[:].rearrange("p b t -> p (b t)"),
+                )
+            acc = acc_psum.tile([P, CHUNK], F32, name="acc")
+            for g in range(PASSES):
+                cols = slice(g * FEATURES, (g + 1) * FEATURES)
+                nc.tensor.matmul_mx(
+                    out=acc[:],
+                    lhsT=w_codes[:, cols].bitcast(FP8X4),
+                    lhsT_scale=w_scales[:, cols],
+                    rhs=codes[:, g, :].bitcast(FP8X4),
+                    rhs_scale=scales[:, g, :],
+                    start=(g == 0),
+                    stop=(g == PASSES - 1),
+                )
+            by_feature = o_pool.tile([P, CHUNK], F32, name="by_feature")
+            nc.scalar.activation(
+                out=by_feature[:], in_=acc[:], func=ACT.Identity, bias=bias[:], scale=1.0
+            )
+            back = back_psum.tile([P, ROW_TILES, FEATURES], F32, name="back")
+            for j in range(ROW_TILES):
+                nc.tensor.transpose(
+                    out=back[:, j, :], in_=by_feature[:, j * P : (j + 1) * P], identity=ident[:]
+                )
+            result = o_pool.tile([P, ROW_TILES, FEATURES], F32, name="result")
+            nc.scalar.copy(out=result[:], in_=back[:])
+            nc.sync.dma_start(
+                out=out[c * CHUNK : (c + 1) * CHUNK, :].rearrange("(p j) f -> p j f", j=ROW_TILES),
+                in_=result[:],
+            )

@@ -211,48 +211,62 @@ def tile_roibaseline_pa_t_kernel(tc, h_enc, enc_gamma, enc_beta, w1, b1, out):
 
         affine.append(scale_and_shift(1))
 
-        for c in range(CHUNKS):
-            codes = q_pool.tile([P, PASSES, CHUNK], U32, name="codes", align_bytes=64)
-            scales = q_pool.tile([P, PASSES, CHUNK], U8, name="scales", align_bytes=64)
-            for g in range(PASSES):
-                y = y_pool.tile([P, 4, CHUNK], F32, name="y")
-                for u in range(2):
-                    bank = xt_psum.tile([P, CHUNK], F32, tag="xt", name="bank_b")
-                    transpose_slab(nc, bank, x_chunks[c], 2 * g + u, ident)
-                    for e in range(2):
-                        t = 2 * u + e
-                        nc.scalar.activation(
-                            out=y[:, t, :],
-                            in_=half(bank, e),
-                            func=ACT.Identity,
-                            bias=affine[g][1][:, t : t + 1],
-                            scale=affine[g][0][:, t : t + 1],
-                        )
-                pairs = c_pool.tile([P, 2, CHUNK, 2], BF16, name="pairs")
-                for u in range(2):
-                    y_by_row = y[:, 2 * u : 2 * u + 2, :].rearrange("p e b -> p b e")
-                    nc.vector.scalar_tensor_tensor(
-                        out=pairs[:, u, :, :],
-                        in0=y_by_row,
-                        scalar=SLOPE,
-                        in1=y_by_row,
-                        op0=ALU.mult,
-                        op1=ALU.max,
+        chunk_codes = {}
+
+        def norm(c, g):
+            y = y_pool.tile([P, 4, CHUNK], F32, name="y")
+            for u in range(2):
+                bank = xt_psum.tile([P, CHUNK], F32, tag="xt", name="bank_b")
+                transpose_slab(nc, bank, x_chunks[c], 2 * g + u, ident)
+                for e in range(2):
+                    t = 2 * u + e
+                    nc.scalar.activation(
+                        out=y[:, t, :],
+                        in_=half(bank, e),
+                        func=ACT.Identity,
+                        bias=affine[g][1][:, t : t + 1],
+                        scale=affine[g][0][:, t : t + 1],
                     )
-                grouped = c_pool.tile([P, CHUNK, 4], BF16, name="grouped", align_bytes=64)
-                nc.vector.tensor_copy(
-                    out=grouped[:].rearrange("p b t -> p (b t)").bitcast(F32).rearrange(
-                        "p (b u) -> p b u", u=2
-                    ),
-                    in_=pairs[:].rearrange("p u b e -> p (u b e)").bitcast(F32).rearrange(
-                        "p (u b) -> p b u", u=2
-                    ),
-                )
-                nc.vector.quantize_mx(
-                    out=codes[:, g, :].bitcast(FP8X4),
-                    scales=scales[:, g, :],
-                    in_=grouped[:].rearrange("p b t -> p (b t)"),
-                )
+            pairs = c_pool.tile([P, 2, CHUNK, 2], BF16, name="pairs")
+            return y, pairs
+
+        def leaky(y, pairs, u):
+            y_by_row = y[:, 2 * u : 2 * u + 2, :].rearrange("p e b -> p b e")
+            nc.vector.scalar_tensor_tensor(
+                out=pairs[:, u, :, :],
+                in0=y_by_row,
+                scalar=SLOPE,
+                in1=y_by_row,
+                op0=ALU.mult,
+                op1=ALU.max,
+            )
+
+        def weave(pairs):
+            grouped = c_pool.tile([P, CHUNK, 4], BF16, name="grouped", align_bytes=64)
+            nc.vector.tensor_copy(
+                out=grouped[:].rearrange("p b t -> p (b t)").bitcast(F32).rearrange(
+                    "p (b u) -> p b u", u=2
+                ),
+                in_=pairs[:].rearrange("p u b e -> p (u b e)").bitcast(F32).rearrange(
+                    "p (u b) -> p b u", u=2
+                ),
+            )
+            return grouped
+
+        def quantise(c, g, grouped):
+            if g == 0:
+                codes = q_pool.tile([P, PASSES, CHUNK], U32, name="codes", align_bytes=64)
+                scales = q_pool.tile([P, PASSES, CHUNK], U8, name="scales", align_bytes=64)
+                chunk_codes[c] = (codes, scales)
+            codes, scales = chunk_codes[c]
+            nc.vector.quantize_mx(
+                out=codes[:, g, :].bitcast(FP8X4),
+                scales=scales[:, g, :],
+                in_=grouped[:].rearrange("p b t -> p (b t)"),
+            )
+
+        def multiply(c):
+            codes, scales = chunk_codes[c]
             acc = acc_psum.tile([P, CHUNK], F32, name="acc")
             for g in range(PASSES):
                 cols = slice(g * FEATURES, (g + 1) * FEATURES)
@@ -280,3 +294,21 @@ def tile_roibaseline_pa_t_kernel(tc, h_enc, enc_gamma, enc_beta, w1, b1, out):
                 out=out[c * CHUNK : (c + 1) * CHUNK, :].rearrange("(p j) f -> p j f", j=ROW_TILES),
                 in_=result[:],
             )
+
+        steps = [(c, g) for c in range(CHUNKS) for g in range(PASSES)]
+        with tc.manual_schedule(engines={mybir.EngineType.DVE}):
+            last_pairs = None
+            for i in range(len(steps) + 1):
+                if i < len(steps):
+                    y, pairs = norm(*steps[i])
+                    leaky(y, pairs, 0)
+                if i > 0:
+                    grouped = weave(last_pairs)
+                if i < len(steps):
+                    leaky(y, pairs, 1)
+                    last_pairs = pairs
+                if i > 0:
+                    c, g = steps[i - 1]
+                    quantise(c, g, grouped)
+                    if g == PASSES - 1:
+                        multiply(c)

@@ -241,9 +241,10 @@ def tile_roibaseline_pa_t_kernel(tc, h_enc, enc_gamma, enc_beta, w1, b1, out):
                 op1=ALU.max,
             )
 
-        def weave(pairs):
+        def weave(i, pairs):
             grouped = c_pool.tile([P, CHUNK, 4], BF16, name="grouped", align_bytes=64)
-            nc.vector.tensor_copy(
+            copy = nc.scalar.copy if i % 3 == 2 else nc.vector.tensor_copy
+            copy(
                 out=grouped[:].rearrange("p b t -> p (b t)").bitcast(F32).rearrange(
                     "p (b u) -> p b u", u=2
                 ),
@@ -297,18 +298,18 @@ def tile_roibaseline_pa_t_kernel(tc, h_enc, enc_gamma, enc_beta, w1, b1, out):
 
         steps = [(c, g) for c in range(CHUNKS) for g in range(PASSES)]
         with tc.manual_schedule(engines={mybir.EngineType.DVE}):
-            last_pairs = None
-            for i in range(len(steps) + 1):
+            pairs = {}
+            grouped = {}
+            for i in range(len(steps) + 2):
                 if i < len(steps):
-                    y, pairs = norm(*steps[i])
-                    leaky(y, pairs, 0)
-                if i > 0:
-                    grouped = weave(last_pairs)
+                    y, pairs[i] = norm(*steps[i])
+                    leaky(y, pairs[i], 0)
+                if 0 < i <= len(steps):
+                    grouped[i - 1] = weave(i - 1, pairs[i - 1])
                 if i < len(steps):
-                    leaky(y, pairs, 1)
-                    last_pairs = pairs
-                if i > 0:
-                    c, g = steps[i - 1]
-                    quantise(c, g, grouped)
+                    leaky(y, pairs[i], 1)
+                if i > 1:
+                    c, g = steps[i - 2]
+                    quantise(c, g, grouped[i - 2])
                     if g == PASSES - 1:
                         multiply(c)

@@ -79,7 +79,7 @@ def tile_roibaseline_pa_t_kernel(tc, h_enc, enc_gamma, enc_beta, w1, b1, out):
             nc.sync.dma_start(
                 out=x_chunk[:],
                 in_=h_enc[c * CHUNK : (c + 1) * CHUNK].rearrange(
-                    "(p j) r o -> p j (r o)", j=ROW_TILES
+                    "(j p) r o -> p j (r o)", j=ROW_TILES
                 ),
             )
             x_chunks.append(x_chunk)
@@ -214,43 +214,31 @@ def tile_roibaseline_pa_t_kernel(tc, h_enc, enc_gamma, enc_beta, w1, b1, out):
         chunk_codes = {}
 
         def norm(c, g):
-            y = y_pool.tile([P, 4, CHUNK], F32, name="y")
+            y = y_pool.tile([P, CHUNK // 4, 4, 4], F32, name="y")
             for u in range(2):
                 bank = xt_psum.tile([P, CHUNK], F32, tag="xt", name="bank_b")
                 transpose_slab(nc, bank, x_chunks[c], 2 * g + u, ident)
                 for e in range(2):
                     t = 2 * u + e
                     nc.scalar.activation(
-                        out=y[:, t, :],
-                        in_=half(bank, e),
+                        out=y[:, :, t, :],
+                        in_=half(bank, e).rearrange("p (q i) -> p q i", i=4),
                         func=ACT.Identity,
                         bias=affine[g][1][:, t : t + 1],
                         scale=affine[g][0][:, t : t + 1],
                     )
-            pairs = c_pool.tile([P, 2, CHUNK, 2], BF16, name="pairs")
-            return y, pairs
+            return y
 
-        def leaky(y, pairs, u):
-            y_by_row = y[:, 2 * u : 2 * u + 2, :].rearrange("p e b -> p b e")
+        def leaky(y):
+            grouped = c_pool.tile([P, 4, CHUNK], BF16, name="grouped", align_bytes=64)
+            y_run = y[:].rearrange("p q t i -> p (q t) i")
             nc.vector.scalar_tensor_tensor(
-                out=pairs[:, u, :, :],
-                in0=y_by_row,
+                out=grouped[:].rearrange("p i k -> p k i"),
+                in0=y_run,
                 scalar=SLOPE,
-                in1=y_by_row,
+                in1=y_run,
                 op0=ALU.mult,
                 op1=ALU.max,
-            )
-
-        def weave(i, pairs):
-            grouped = c_pool.tile([P, CHUNK, 4], BF16, name="grouped", align_bytes=64)
-            copy = nc.scalar.copy if i % 3 == 2 else nc.vector.tensor_copy
-            copy(
-                out=grouped[:].rearrange("p b t -> p (b t)").bitcast(F32).rearrange(
-                    "p (b u) -> p b u", u=2
-                ),
-                in_=pairs[:].rearrange("p u b e -> p (u b e)").bitcast(F32).rearrange(
-                    "p (u b) -> p b u", u=2
-                ),
             )
             return grouped
 
@@ -263,7 +251,7 @@ def tile_roibaseline_pa_t_kernel(tc, h_enc, enc_gamma, enc_beta, w1, b1, out):
             nc.vector.quantize_mx(
                 out=codes[:, g, :].bitcast(FP8X4),
                 scales=scales[:, g, :],
-                in_=grouped[:].rearrange("p b t -> p (b t)"),
+                in_=grouped[:].rearrange("p i k -> p (i k)"),
             )
 
         def multiply(c):
@@ -298,18 +286,12 @@ def tile_roibaseline_pa_t_kernel(tc, h_enc, enc_gamma, enc_beta, w1, b1, out):
 
         steps = [(c, g) for c in range(CHUNKS) for g in range(PASSES)]
         with tc.manual_schedule(engines={mybir.EngineType.DVE}):
-            pairs = {}
             grouped = {}
-            for i in range(len(steps) + 2):
+            for i in range(len(steps) + 1):
                 if i < len(steps):
-                    y, pairs[i] = norm(*steps[i])
-                    leaky(y, pairs[i], 0)
-                if 0 < i <= len(steps):
-                    grouped[i - 1] = weave(i - 1, pairs[i - 1])
-                if i < len(steps):
-                    leaky(y, pairs[i], 1)
-                if i > 1:
-                    c, g = steps[i - 2]
-                    quantise(c, g, grouped[i - 2])
+                    grouped[i] = leaky(norm(*steps[i]))
+                if i > 0:
+                    c, g = steps[i - 1]
+                    quantise(c, g, grouped[i - 1])
                     if g == PASSES - 1:
                         multiply(c)

@@ -29,11 +29,13 @@ BN_WIDTH = 512
 BN_CALLS = 2 * CHUNK // BN_WIDTH
 BN_SLOTS = CHUNKS * BN_CALLS
 
+LATE_BANKS = [(c, 2) for c in range(CHUNKS) if c % 5 in (1, 3)]
+
 FLOPS = 2 * BATCH * CHANNELS * FEATURES
 
 
 def scalar_takes(c, s):
-    return s == 3 or (s == 2 and c % 2 == 0)
+    return s >= 2 and (c, s) not in LATE_BANKS[0::2]
 
 
 def transpose_slab(nc, bank, x_chunk, slab, ident):
@@ -59,10 +61,12 @@ def tile_roibaseline_pa_t_kernel(tc, h_enc, enc_gamma, enc_beta, w1, b1, out):
         c_pool = ctx.enter_context(tc.tile_pool(name="c", bufs=3))
         q_pool = ctx.enter_context(tc.tile_pool(name="q", bufs=3))
         o_pool = ctx.enter_context(tc.tile_pool(name="o", bufs=3))
-        xt_psum = ctx.enter_context(tc.psum_pool(name="xt", bufs=4))
-        acc_psum = ctx.enter_context(tc.psum_pool(name="acc", bufs=2))
+        xt_psum = [
+            ctx.enter_context(tc.psum_pool(name="xt0", bufs=3)),
+            ctx.enter_context(tc.psum_pool(name="xt1", bufs=3)),
+        ]
+        acc_psum = ctx.enter_context(tc.psum_pool(name="acc", bufs=1))
         back_psum = ctx.enter_context(tc.psum_pool(name="back", bufs=1))
-        sum_psum = ctx.enter_context(tc.psum_pool(name="sum", bufs=1))
 
         ident = keep.tile([P, P], F32, name="ident")
         make_identity(nc, ident[:])
@@ -76,12 +80,13 @@ def tile_roibaseline_pa_t_kernel(tc, h_enc, enc_gamma, enc_beta, w1, b1, out):
         x_chunks = []
         for c in range(CHUNKS):
             x_chunk = keep.tile([P, ROW_TILES, CHANNELS], BF16, name="x%d" % c)
-            nc.sync.dma_start(
-                out=x_chunk[:],
-                in_=h_enc[c * CHUNK : (c + 1) * CHUNK].rearrange(
-                    "(j p) r o -> p j (r o)", j=ROW_TILES
-                ),
+            chunk_rows = h_enc[c * CHUNK : (c + 1) * CHUNK].rearrange(
+                "(j p) r o -> p j (r o)", j=ROW_TILES
             )
+            pieces = ROW_TILES if c == 0 else 1
+            width = ROW_TILES // pieces
+            for j in range(0, ROW_TILES, width):
+                nc.sync.dma_start(out=x_chunk[:, j : j + width, :], in_=chunk_rows[:, j : j + width, :])
             x_chunks.append(x_chunk)
         gamma_bf = keep.tile([P, PASSES, 4], BF16, name="gamma_bf")
         beta_bf = keep.tile([P, PASSES, 4], BF16, name="beta_bf")
@@ -96,71 +101,85 @@ def tile_roibaseline_pa_t_kernel(tc, h_enc, enc_gamma, enc_beta, w1, b1, out):
         )
         nc.sync.dma_start(out=bias_bf[:], in_=b1.rearrange("(f o) -> f o", o=1))
 
-        w_bank = xt_psum.tile([P, SLABS * P], F32, tag="xt", name="w_bank")
-        for s in range(SLABS):
-            first = 256 * (s // 2) + s % 2
-            nc.tensor.transpose(
-                out=w_bank[:, s * P : (s + 1) * P],
-                in_=w_rows[:].bitcast(F32)[:, first : first + 2 * P - 1 : 2],
-                identity=ident[:],
-            )
-        w_grouped = keep.tile([P, PASSES * FEATURES * 4], BF16, name="w_grouped", align_bytes=64)
-        nc.vector.tensor_copy(
-            out=w_grouped[:].bitcast(F32).rearrange("p (g f u) -> p g f u", g=PASSES, u=2),
-            in_=w_bank[:].rearrange("p (g u f) -> p g f u", g=PASSES, u=2),
-        )
         w_codes = keep.tile([P, PASSES * FEATURES], U32, name="w_codes", align_bytes=64)
         w_scales = keep.tile([P, PASSES * FEATURES], U8, name="w_scales", align_bytes=64)
-        nc.vector.quantize_mx(out=w_codes[:].bitcast(FP8X4), scales=w_scales[:], in_=w_grouped[:])
+
+        def prepare_w():
+            w_bank = acc_psum.tile([P, SLABS * P], F32, tag="acc", name="w_bank")
+            for s in range(SLABS):
+                first = 256 * (s // 2) + s % 2
+                nc.tensor.transpose(
+                    out=w_bank[:, s * P : (s + 1) * P],
+                    in_=w_rows[:].bitcast(F32)[:, first : first + 2 * P - 1 : 2],
+                    identity=ident[:],
+                )
+            w_grouped = keep.tile([P, PASSES * FEATURES * 4], BF16, name="w_grouped", align_bytes=64)
+            nc.vector.tensor_copy(
+                out=w_grouped[:].bitcast(F32).rearrange("p (g f u) -> p g f u", g=PASSES, u=2),
+                in_=w_bank[:].rearrange("p (g u f) -> p g f u", g=PASSES, u=2),
+            )
+            nc.vector.quantize_mx(out=w_codes[:].bitcast(FP8X4), scales=w_scales[:], in_=w_grouped[:])
 
         bn_parts = keep.tile([P, SLABS, 1 + BN_SLOTS, 6], F32, name="bn_parts")
         neg_x0 = keep.tile([P, 2, 2], F32, name="neg_x0")
         sq_parts = keep.tile([P, 2, 2, CHUNKS], F32, name="sq_parts")
-        sum_parts = sum_psum.tile([P, 2, 2, CHUNKS], F32, name="sum_parts")
+        sum_parts = back_psum.tile([P, 2, 2, CHUNKS], F32, tag="back", name="sum_parts")
         bn_used = [1, 1, 1, 1]
-        for c in range(CHUNKS):
-            for s in range(SLABS):
-                bank = xt_psum.tile([P, CHUNK], F32, tag="xt", name="bank_a")
-                transpose_slab(nc, bank, x_chunks[c], s, ident)
-                if not scalar_takes(c, s):
-                    for h in range(BN_CALLS):
-                        nc.vector.bn_stats(
-                            out=bn_parts[:, s, bn_used[s], :],
-                            in_=bank[:].bitcast(BF16)[:, h * BN_WIDTH : (h + 1) * BN_WIDTH],
-                        )
-                        bn_used[s] += 1
-                    continue
-                u = s - 2
-                if c == 0:
-                    nc.scalar.mul(
-                        out=neg_x0[:, u, :], in_=bank[:].bitcast(BF16)[:, 0:2], mul=-1.0
+        sums = []
+        scalar_used = [0, 0]
+        rows = keep.tile([P, 2, 2], F32, name="rows")
+        per_row = keep.tile([P, 2, 2], F32, name="per_row")
+        for u in range(2):
+            banks = sum(1 for c in range(CHUNKS) if scalar_takes(c, 2 + u))
+            nc.vector.memset(rows[:, u, :], float(banks * CHUNK))
+        nc.vector.reciprocal(out=per_row[:], in_=rows[:])
+
+        def statistics(c, s):
+            on_scalar = scalar_takes(c, s)
+            bank = xt_psum[on_scalar].tile([P, CHUNK], F32, tag="xt", name="bank_a")
+            transpose_slab(nc, bank, x_chunks[c], s, ident)
+            if not on_scalar:
+                for h in range(BN_CALLS):
+                    nc.vector.bn_stats(
+                        out=bn_parts[:, s, bn_used[s], :],
+                        in_=bank[:].bitcast(BF16)[:, h * BN_WIDTH : (h + 1) * BN_WIDTH],
                     )
+                    bn_used[s] += 1
+                return
+            u = s - 2
+            col = scalar_used[u]
+            scalar_used[u] += 1
+            sums.append((c, u, col))
+            if c == 0:
+                nc.scalar.mul(out=neg_x0[:, u, :], in_=bank[:].bitcast(BF16)[:, 0:2], mul=-1.0)
+            for e in range(2):
+                junk = junk_pool.tile([P, CHUNK], BF16, name="junk")
+                nc.scalar.activation(
+                    out=junk[:],
+                    in_=half(bank, e),
+                    func=ACT.Square,
+                    bias=neg_x0[:, u, e : e + 1],
+                    scale=1.0,
+                    accum_out=sq_parts[:, u, e, col : col + 1],
+                )
+
+        def add_up():
+            for c, u, col in sums:
                 for e in range(2):
-                    junk = junk_pool.tile([P, CHUNK], BF16, name="junk")
-                    nc.scalar.activation(
-                        out=junk[:],
-                        in_=half(bank, e),
-                        func=ACT.Square,
-                        bias=neg_x0[:, u, e : e + 1],
-                        scale=1.0,
-                        accum_out=sq_parts[:, u, e, c : c + 1],
-                    )
                     first = 512 + 2 * u + e
                     for j in range(ROW_TILES):
                         nc.tensor.matmul(
-                            out=sum_parts[:, u, e, c : c + 1],
+                            out=sum_parts[:, u, e, col : col + 1],
                             lhsT=x_chunks[c][:, j, first : first + 4 * P - 3 : 4],
                             rhs=ones[:],
                             start=(j == 0),
                             stop=(j == ROW_TILES - 1),
                         )
+            sums.clear()
 
         gamma = keep.tile([P, SLABS * 2], F32, name="gamma")
         beta = keep.tile([P, SLABS * 2], F32, name="beta")
         bias = keep.tile([P, 1], F32, name="bias")
-        nc.vector.tensor_copy(out=gamma[:], in_=gamma_bf[:].rearrange("p g t -> p (g t)"))
-        nc.vector.tensor_copy(out=beta[:], in_=beta_bf[:].rearrange("p g t -> p (g t)"))
-        nc.vector.tensor_copy(out=bias[:], in_=bias_bf[:])
 
         def scale_and_shift(g):
             mean_var = keep.tile([P, 4, 2], F32, name="mean_var%d" % g)
@@ -174,75 +193,104 @@ def tile_roibaseline_pa_t_kernel(tc, h_enc, enc_gamma, enc_beta, w1, b1, out):
                 )
             scale = keep.tile([P, 4], F32, name="scale%d" % g)
             shift = keep.tile([P, 4], F32, name="shift%d" % g)
-            nc.vector.tensor_scalar_add(out=scale[:], in0=mean_var[:, :, 1], scalar1=EPS)
+            cols = slice(4 * g, 4 * g + 4)
+            nc.gpsimd.tensor_scalar(
+                out=scale[:], in0=mean_var[:, :, 1], scalar1=EPS, scalar2=None, op0=ALU.add
+            )
             nc.gpsimd.tensor_tensor(out=scale[:], in0=scale[:], in1=minus_half[:], op=ALU.pow)
-            nc.vector.tensor_mul(out=scale[:], in0=scale[:], in1=gamma[:, 4 * g : 4 * g + 4])
-            nc.vector.tensor_mul(out=shift[:], in0=mean_var[:, :, 0], in1=scale[:])
-            nc.vector.tensor_sub(out=shift[:], in0=beta[:, 4 * g : 4 * g + 4], in1=shift[:])
+            nc.gpsimd.tensor_tensor(out=scale[:], in0=scale[:], in1=gamma[:, cols], op=ALU.mult)
+            nc.gpsimd.tensor_tensor(
+                out=shift[:], in0=mean_var[:, :, 0], in1=scale[:], op=ALU.mult
+            )
+            nc.gpsimd.tensor_tensor(
+                out=shift[:], in0=beta[:, cols], in1=shift[:], op=ALU.subtract
+            )
             return scale, shift
 
-        affine = [scale_and_shift(0)]
+        engines = {mybir.EngineType.PE, mybir.EngineType.Activation, mybir.EngineType.DVE}
+        with tc.manual_schedule(engines=engines):
+            for c in range(CHUNKS):
+                for s in (0, 2, 1, 3):
+                    if (c, s) not in LATE_BANKS:
+                        statistics(c, s)
+                add_up()
+                if c == 1:
+                    prepare_w()
+            nc.gpsimd.tensor_copy(out=gamma[:], in_=gamma_bf[:].rearrange("p g t -> p (g t)"))
+            nc.gpsimd.tensor_copy(out=beta[:], in_=beta_bf[:].rearrange("p g t -> p (g t)"))
+            nc.gpsimd.tensor_copy(out=bias[:], in_=bias_bf[:])
+            affine = [scale_and_shift(0)]
+            for bank in LATE_BANKS:
+                statistics(*bank)
+            add_up()
 
-        x_sum = keep.tile([P, 2, 2], F32, name="x_sum")
-        sq_sum = keep.tile([P, 2, 2], F32, name="sq_sum")
-        off = keep.tile([P, 2, 2], F32, name="off")
-        for u in range(2):
-            step = 2 - u
-            rows = float(BATCH // step)
-            share = bn_parts[:, 2 + u, 0, :].rearrange("p (e k) -> p e k", k=3)
-            nc.vector.memset(share[:, :, 0], rows)
-            nc.vector.tensor_reduce(
-                out=x_sum[:, u, :], in_=sum_parts[:, u, :, 0:CHUNKS:step], axis=AXIS_X, op=ALU.add
-            )
-            nc.vector.tensor_reduce(
-                out=sq_sum[:, u, :], in_=sq_parts[:, u, :, 0:CHUNKS:step], axis=AXIS_X, op=ALU.add
-            )
-            nc.vector.tensor_scalar_mul(out=share[:, :, 1], in0=x_sum[:, u, :], scalar1=1.0 / rows)
-            nc.vector.tensor_add(out=off[:, u, :], in0=share[:, :, 1], in1=neg_x0[:, u, :])
-            nc.vector.tensor_mul(out=off[:, u, :], in0=off[:, u, :], in1=off[:, u, :])
-            nc.vector.scalar_tensor_tensor(
-                out=share[:, :, 2],
-                in0=off[:, u, :],
-                scalar=-rows,
-                in1=sq_sum[:, u, :],
-                op0=ALU.mult,
-                op1=ALU.add,
-            )
-
-        affine.append(scale_and_shift(1))
-
-        chunk_codes = {}
-
-        def norm(c, g):
-            y = y_pool.tile([P, CHUNK // 4, 4, 4], F32, name="y")
+            x_sum = keep.tile([P, 2, 2], F32, name="x_sum")
+            sq_sum = keep.tile([P, 2, 2], F32, name="sq_sum")
+            off = keep.tile([P, 2, 2], F32, name="off")
+            share = bn_parts[:, 2:4, 0, :].rearrange("p u (e k) -> p u e k", k=3)
             for u in range(2):
-                bank = xt_psum.tile([P, CHUNK], F32, tag="xt", name="bank_b")
-                transpose_slab(nc, bank, x_chunks[c], 2 * g + u, ident)
-                for e in range(2):
-                    t = 2 * u + e
-                    nc.scalar.activation(
-                        out=y[:, :, t, :],
-                        in_=half(bank, e).rearrange("p (q i) -> p q i", i=4),
-                        func=ACT.Identity,
-                        bias=affine[g][1][:, t : t + 1],
-                        scale=affine[g][0][:, t : t + 1],
-                    )
-            return y
+                used = scalar_used[u]
+                nc.vector.tensor_reduce(
+                    out=x_sum[:, u, :], in_=sum_parts[:, u, :, 0:used], axis=AXIS_X, op=ALU.add
+                )
+                nc.vector.tensor_reduce(
+                    out=sq_sum[:, u, :], in_=sq_parts[:, u, :, 0:used], axis=AXIS_X, op=ALU.add
+                )
+            nc.vector.tensor_copy(out=share[:, :, :, 0], in_=rows[:])
+            nc.vector.tensor_mul(out=share[:, :, :, 1], in0=x_sum[:], in1=per_row[:])
+            nc.vector.tensor_add(out=off[:], in0=share[:, :, :, 1], in1=neg_x0[:])
+            nc.vector.tensor_mul(out=off[:], in0=off[:], in1=off[:])
+            nc.vector.tensor_mul(out=off[:], in0=off[:], in1=rows[:])
+            nc.vector.tensor_sub(out=share[:, :, :, 2], in0=sq_sum[:], in1=off[:])
+            affine.append(scale_and_shift(1))
 
-        def leaky(y):
-            grouped = c_pool.tile([P, 4, CHUNK], BF16, name="grouped", align_bytes=64)
-            y_run = y[:].rearrange("p q t i -> p (q t) i")
+        steps = [(0, 0), (1, 0), (0, 1), (1, 1)]
+        steps += [(c, g) for c in range(2, CHUNKS) for g in range(PASSES)]
+        banks = {}
+        normed = {}
+        grouped = {}
+        chunk_codes = {}
+        by_feature = {}
+        turned = {}
+
+        def turn(i):
+            c, g = steps[i]
+            banks[i] = []
+            for u in range(2):
+                bank = xt_psum[u].tile([P, CHUNK], F32, tag="xt", name="bank_b")
+                transpose_slab(nc, bank, x_chunks[c], 2 * g + u, ident)
+                banks[i].append(bank)
+
+        def norm(i, u):
+            g = steps[i][1]
+            if u == 0:
+                y = y_pool.tile([P, CHUNK // 4, 4, 4], F32, name="y")
+                normed[i] = y
+            for e in range(2):
+                t = 2 * u + e
+                nc.scalar.activation(
+                    out=normed[i][:, :, t, :],
+                    in_=half(banks[i][u], e).rearrange("p (q i) -> p q i", i=4),
+                    func=ACT.Identity,
+                    bias=affine[g][1][:, t : t + 1],
+                    scale=affine[g][0][:, t : t + 1],
+                )
+
+        def leaky(i):
+            woven = c_pool.tile([P, 4, CHUNK], BF16, name="woven", align_bytes=64)
+            y_run = normed[i][:].rearrange("p q t i -> p (q t) i")
             nc.vector.scalar_tensor_tensor(
-                out=grouped[:].rearrange("p i k -> p k i"),
+                out=woven[:].rearrange("p i k -> p k i"),
                 in0=y_run,
                 scalar=SLOPE,
                 in1=y_run,
                 op0=ALU.mult,
                 op1=ALU.max,
             )
-            return grouped
+            grouped[i] = woven
 
-        def quantise(c, g, grouped):
+        def quantise(i):
+            c, g = steps[i]
             if g == 0:
                 codes = q_pool.tile([P, PASSES, CHUNK], U32, name="codes", align_bytes=64)
                 scales = q_pool.tile([P, PASSES, CHUNK], U8, name="scales", align_bytes=64)
@@ -251,12 +299,12 @@ def tile_roibaseline_pa_t_kernel(tc, h_enc, enc_gamma, enc_beta, w1, b1, out):
             nc.vector.quantize_mx(
                 out=codes[:, g, :].bitcast(FP8X4),
                 scales=scales[:, g, :],
-                in_=grouped[:].rearrange("p i k -> p (i k)"),
+                in_=grouped[i][:].rearrange("p i k -> p (i k)"),
             )
 
         def multiply(c):
             codes, scales = chunk_codes[c]
-            acc = acc_psum.tile([P, CHUNK], F32, name="acc")
+            acc = acc_psum.tile([P, CHUNK], F32, tag="acc", name="acc")
             for g in range(PASSES):
                 cols = slice(g * FEATURES, (g + 1) * FEATURES)
                 nc.tensor.matmul_mx(
@@ -268,30 +316,51 @@ def tile_roibaseline_pa_t_kernel(tc, h_enc, enc_gamma, enc_beta, w1, b1, out):
                     start=(g == 0),
                     stop=(g == PASSES - 1),
                 )
-            by_feature = o_pool.tile([P, CHUNK], F32, name="by_feature")
+            by_feature[c] = acc
+
+        def add_bias(c):
+            biased = o_pool.tile([P, CHUNK], F32, name="biased")
             nc.scalar.activation(
-                out=by_feature[:], in_=acc[:], func=ACT.Identity, bias=bias[:], scale=1.0
+                out=biased[:], in_=by_feature[c][:], func=ACT.Identity, bias=bias[:], scale=1.0
             )
-            back = back_psum.tile([P, ROW_TILES, FEATURES], F32, name="back")
+            back = back_psum.tile([P, ROW_TILES, FEATURES], F32, tag="back", name="back")
             for j in range(ROW_TILES):
                 nc.tensor.transpose(
-                    out=back[:, j, :], in_=by_feature[:, j * P : (j + 1) * P], identity=ident[:]
+                    out=back[:, j, :], in_=biased[:, j * P : (j + 1) * P], identity=ident[:]
                 )
+            turned[c] = back
+
+        def store(c):
             result = o_pool.tile([P, ROW_TILES, FEATURES], F32, name="result")
-            nc.scalar.copy(out=result[:], in_=back[:])
+            nc.scalar.copy(out=result[:], in_=turned[c][:])
             nc.sync.dma_start(
                 out=out[c * CHUNK : (c + 1) * CHUNK, :].rearrange("(p j) f -> p j f", j=ROW_TILES),
                 in_=result[:],
             )
 
-        steps = [(c, g) for c in range(CHUNKS) for g in range(PASSES)]
-        with tc.manual_schedule(engines={mybir.EngineType.DVE}):
-            grouped = {}
-            for i in range(len(steps) + 1):
-                if i < len(steps):
-                    grouped[i] = leaky(norm(*steps[i]))
-                if i > 0:
+        last = len(steps)
+        done = {}
+        with tc.manual_schedule(engines=engines):
+            turn(0)
+            turn(1)
+            norm(0, 0)
+            norm(0, 1)
+            for i in range(last + 3):
+                if i + 2 < last:
+                    turn(i + 2)
+                if i + 1 < last:
+                    norm(i + 1, 0)
+                if i - 1 in done:
+                    add_bias(done[i - 1])
+                if i - 2 in done:
+                    store(done[i - 2])
+                if i + 1 < last:
+                    norm(i + 1, 1)
+                if i < last:
+                    leaky(i)
+                if 0 < i <= last:
+                    quantise(i - 1)
                     c, g = steps[i - 1]
-                    quantise(c, g, grouped[i - 1])
                     if g == PASSES - 1:
                         multiply(c)
+                        done[i] = c

@@ -29,13 +29,13 @@ BN_WIDTH = 512
 BN_CALLS = 2 * CHUNK // BN_WIDTH
 BN_SLOTS = CHUNKS * BN_CALLS
 
-LATE_BANKS = [(c, 2) for c in range(CHUNKS) if c % 5 in (1, 3)]
+LATE_BANKS = [(c, 2) for c in range(1, CHUNKS, 2)]
 
 FLOPS = 2 * BATCH * CHANNELS * FEATURES
 
 
 def scalar_takes(c, s):
-    return s >= 2 and (c, s) not in LATE_BANKS[0::2]
+    return s >= 2 and ((c, s) not in LATE_BANKS or (c, s) in LATE_BANKS[2::3])
 
 
 def transpose_slab(nc, bank, x_chunk, slab, ident):
@@ -57,7 +57,7 @@ def tile_roibaseline_pa_t_kernel(tc, h_enc, enc_gamma, enc_beta, w1, b1, out):
     with ExitStack() as ctx:
         keep = ctx.enter_context(tc.tile_pool(name="keep", bufs=1))
         junk_pool = ctx.enter_context(tc.tile_pool(name="junk", bufs=4))
-        y_pool = ctx.enter_context(tc.tile_pool(name="y", bufs=3))
+        y_pool = ctx.enter_context(tc.tile_pool(name="y", bufs=4))
         c_pool = ctx.enter_context(tc.tile_pool(name="c", bufs=3))
         q_pool = ctx.enter_context(tc.tile_pool(name="q", bufs=3))
         o_pool = ctx.enter_context(tc.tile_pool(name="o", bufs=3))
@@ -341,22 +341,17 @@ def tile_roibaseline_pa_t_kernel(tc, h_enc, enc_gamma, enc_beta, w1, b1, out):
         last = len(steps)
         done = {}
         with tc.manual_schedule(engines=engines):
-            turn(0)
-            turn(1)
-            norm(0, 0)
-            norm(0, 1)
-            for i in range(last + 3):
-                if i + 2 < last:
-                    turn(i + 2)
-                if i + 1 < last:
-                    norm(i + 1, 0)
+            for i in range(-3, last + 3):
+                if i + 3 < last:
+                    turn(i + 3)
+                if 0 <= i + 2 < last:
+                    norm(i + 2, 0)
+                    norm(i + 2, 1)
                 if i - 1 in done:
                     add_bias(done[i - 1])
                 if i - 2 in done:
                     store(done[i - 2])
-                if i + 1 < last:
-                    norm(i + 1, 1)
-                if i < last:
+                if 0 <= i < last:
                     leaky(i)
                 if 0 < i <= last:
                     quantise(i - 1)

@@ -81,7 +81,7 @@ def tile_roibaseline_pa_t_kernel(tc, h_enc, enc_gamma, enc_beta, w1, b1, out):
         for c in range(CHUNKS):
             x_chunk = keep.tile([P, ROW_TILES, CHANNELS], BF16, name="x%d" % c)
             chunk_rows = h_enc[c * CHUNK : (c + 1) * CHUNK].rearrange(
-                "(j p) r o -> p j (r o)", j=ROW_TILES
+                "(p j) r o -> p j (r o)", j=ROW_TILES
             )
             pieces = ROW_TILES if c == 0 else 1
             width = ROW_TILES // pieces
@@ -270,7 +270,7 @@ def tile_roibaseline_pa_t_kernel(tc, h_enc, enc_gamma, enc_beta, w1, b1, out):
                 t = 2 * u + e
                 nc.scalar.activation(
                     out=normed[i][:, :, t, :],
-                    in_=half(banks[i][u], e).rearrange("p (q i) -> p q i", i=4),
+                    in_=half(banks[i][u], e).rearrange("p (i q) -> p q i", i=4),
                     func=ACT.Identity,
                     bias=affine[g][1][:, t : t + 1],
                     scale=affine[g][0][:, t : t + 1],

@@ -38,12 +38,11 @@ def scalar_takes(c, s):
     return s >= 2 and ((c, s) not in LATE_BANKS or (c, s) in LATE_BANKS[2::3])
 
 
-def transpose_slab(nc, bank, x_chunk, slab, ident):
-    first = 256 * (slab // 2) + slab % 2
+def transpose_words(nc, bank, x_chunk, first, step, ident):
     for j in range(ROW_TILES):
         nc.tensor.transpose(
             out=bank[:, j * P : (j + 1) * P],
-            in_=x_chunk[:, j, :].bitcast(F32)[:, first : first + 2 * P - 1 : 2],
+            in_=x_chunk[:, j, :].bitcast(F32)[:, first : first + step * (P - 1) + 1 : step],
             identity=ident[:],
         )
 
@@ -59,7 +58,7 @@ def tile_roibaseline_pa_t_kernel(tc, h_enc, enc_gamma, enc_beta, w1, b1, out):
         junk_pool = ctx.enter_context(tc.tile_pool(name="junk", bufs=4))
         y_pool = ctx.enter_context(tc.tile_pool(name="y", bufs=4))
         c_pool = ctx.enter_context(tc.tile_pool(name="c", bufs=3))
-        q_pool = ctx.enter_context(tc.tile_pool(name="q", bufs=3))
+        q_pool = ctx.enter_context(tc.tile_pool(name="q", bufs=5))
         o_pool = ctx.enter_context(tc.tile_pool(name="o", bufs=3))
         xt_psum = [
             ctx.enter_context(tc.psum_pool(name="xt0", bufs=3)),
@@ -72,6 +71,9 @@ def tile_roibaseline_pa_t_kernel(tc, h_enc, enc_gamma, enc_beta, w1, b1, out):
         make_identity(nc, ident[:])
         ones = keep.tile([P, 1], BF16, name="ones")
         nc.vector.memset(ones[:], 1.0)
+        wide_ident = keep.tile([P, 3 * P], F32, name="wide_ident")
+        nc.gpsimd.memset(wide_ident[:], 0.0)
+        nc.gpsimd.tensor_copy(out=wide_ident[:, P : 2 * P], in_=ident[:])
         minus_half = keep.tile([P, 4], F32, name="minus_half")
         nc.vector.memset(minus_half[:], -0.5)
 
@@ -137,7 +139,7 @@ def tile_roibaseline_pa_t_kernel(tc, h_enc, enc_gamma, enc_beta, w1, b1, out):
         def statistics(c, s):
             on_scalar = scalar_takes(c, s)
             bank = xt_psum[on_scalar].tile([P, CHUNK], F32, tag="xt", name="bank_a")
-            transpose_slab(nc, bank, x_chunks[c], s, ident)
+            transpose_words(nc, bank, x_chunks[c], s * P, 1, ident)
             if not on_scalar:
                 for h in range(BN_CALLS):
                     nc.vector.bn_stats(
@@ -166,11 +168,11 @@ def tile_roibaseline_pa_t_kernel(tc, h_enc, enc_gamma, enc_beta, w1, b1, out):
         def add_up():
             for c, u, col in sums:
                 for e in range(2):
-                    first = 512 + 2 * u + e
+                    first = 256 * (2 + u) + e
                     for j in range(ROW_TILES):
                         nc.tensor.matmul(
                             out=sum_parts[:, u, e, col : col + 1],
-                            lhsT=x_chunks[c][:, j, first : first + 4 * P - 3 : 4],
+                            lhsT=x_chunks[c][:, j, first : first + 2 * P - 1 : 2],
                             rhs=ones[:],
                             start=(j == 0),
                             stop=(j == ROW_TILES - 1),
@@ -181,27 +183,44 @@ def tile_roibaseline_pa_t_kernel(tc, h_enc, enc_gamma, enc_beta, w1, b1, out):
         beta = keep.tile([P, SLABS * 2], F32, name="beta")
         bias = keep.tile([P, 1], F32, name="bias")
 
-        def scale_and_shift(g):
-            mean_var = keep.tile([P, 4, 2], F32, name="mean_var%d" % g)
-            for t in range(4):
-                s = 2 * g + t // 2
-                e = t % 2
+        def aggregate(g):
+            mean_var = keep.tile([P, 2, 2, 2], F32, name="mean_var%d" % g)
+            for h in range(2):
+                s = 2 * g + h
                 first_slot = 0 if s >= 2 else 1
-                nc.vector.bn_aggr(
-                    out=mean_var[:, t, :],
-                    in_=bn_parts[:, s, first_slot : bn_used[s], 3 * e : 3 * e + 3],
-                )
+                for e in range(2):
+                    nc.vector.bn_aggr(
+                        out=mean_var[:, h, e, :],
+                        in_=bn_parts[:, s, first_slot : bn_used[s], 3 * e : 3 * e + 3],
+                    )
+            return mean_var
+
+        def reorder(g, mean_var):
+            by_pass = acc_psum.tile([P, 2, 2, 2], F32, tag="acc", name="by_pass")
+            for u in range(2):
+                for h in range(2):
+                    first = P + u - P * h
+                    nc.tensor.matmul(
+                        out=by_pass[:, u, :, :],
+                        lhsT=wide_ident[:, first : first + 2 * P - 1 : 2],
+                        rhs=mean_var[:, h, :, :],
+                        start=(h == 0),
+                        stop=(h == 1),
+                    )
+            return by_pass
+
+        def scale_and_shift(g, by_pass):
+            moments = keep.tile([P, 4, 2], F32, name="moments%d" % g)
+            nc.vector.tensor_copy(out=moments[:], in_=by_pass[:].rearrange("p u e m -> p (u e) m"))
             scale = keep.tile([P, 4], F32, name="scale%d" % g)
             shift = keep.tile([P, 4], F32, name="shift%d" % g)
             cols = slice(4 * g, 4 * g + 4)
             nc.gpsimd.tensor_scalar(
-                out=scale[:], in0=mean_var[:, :, 1], scalar1=EPS, scalar2=None, op0=ALU.add
+                out=scale[:], in0=moments[:, :, 1], scalar1=EPS, scalar2=None, op0=ALU.add
             )
             nc.gpsimd.tensor_tensor(out=scale[:], in0=scale[:], in1=minus_half[:], op=ALU.pow)
             nc.gpsimd.tensor_tensor(out=scale[:], in0=scale[:], in1=gamma[:, cols], op=ALU.mult)
-            nc.gpsimd.tensor_tensor(
-                out=shift[:], in0=mean_var[:, :, 0], in1=scale[:], op=ALU.mult
-            )
+            nc.gpsimd.tensor_tensor(out=shift[:], in0=moments[:, :, 0], in1=scale[:], op=ALU.mult)
             nc.gpsimd.tensor_tensor(
                 out=shift[:], in0=beta[:, cols], in1=shift[:], op=ALU.subtract
             )
@@ -219,8 +238,12 @@ def tile_roibaseline_pa_t_kernel(tc, h_enc, enc_gamma, enc_beta, w1, b1, out):
             nc.gpsimd.tensor_copy(out=gamma[:], in_=gamma_bf[:].rearrange("p g t -> p (g t)"))
             nc.gpsimd.tensor_copy(out=beta[:], in_=beta_bf[:].rearrange("p g t -> p (g t)"))
             nc.gpsimd.tensor_copy(out=bias[:], in_=bias_bf[:])
-            affine = [scale_and_shift(0)]
-            for bank in LATE_BANKS:
+            mean_var = aggregate(0)
+            for bank in LATE_BANKS[:3]:
+                statistics(*bank)
+            by_pass = reorder(0, mean_var)
+            affine = [scale_and_shift(0, by_pass)]
+            for bank in LATE_BANKS[3:]:
                 statistics(*bank)
             add_up()
 
@@ -242,10 +265,10 @@ def tile_roibaseline_pa_t_kernel(tc, h_enc, enc_gamma, enc_beta, w1, b1, out):
             nc.vector.tensor_mul(out=off[:], in0=off[:], in1=off[:])
             nc.vector.tensor_mul(out=off[:], in0=off[:], in1=rows[:])
             nc.vector.tensor_sub(out=share[:, :, :, 2], in0=sq_sum[:], in1=off[:])
-            affine.append(scale_and_shift(1))
+            mean_var = aggregate(1)
 
-        steps = [(0, 0), (1, 0), (0, 1), (1, 1)]
-        steps += [(c, g) for c in range(2, CHUNKS) for g in range(PASSES)]
+        steps = [(c, g) for g in range(PASSES) for c in range(4)]
+        steps += [(c, g) for c in range(4, CHUNKS) for g in range(PASSES)]
         banks = {}
         normed = {}
         grouped = {}
@@ -258,7 +281,7 @@ def tile_roibaseline_pa_t_kernel(tc, h_enc, enc_gamma, enc_beta, w1, b1, out):
             banks[i] = []
             for u in range(2):
                 bank = xt_psum[u].tile([P, CHUNK], F32, tag="xt", name="bank_b")
-                transpose_slab(nc, bank, x_chunks[c], 2 * g + u, ident)
+                transpose_words(nc, bank, x_chunks[c], 256 * g + u, 2, ident)
                 banks[i].append(bank)
 
         def norm(i, u):
@@ -344,6 +367,8 @@ def tile_roibaseline_pa_t_kernel(tc, h_enc, enc_gamma, enc_beta, w1, b1, out):
             for i in range(-3, last + 3):
                 if i + 3 < last:
                     turn(i + 3)
+                if i == 0:
+                    by_pass = reorder(1, mean_var)
                 if 0 <= i + 2 < last:
                     norm(i + 2, 0)
                     norm(i + 2, 1)
@@ -353,6 +378,8 @@ def tile_roibaseline_pa_t_kernel(tc, h_enc, enc_gamma, enc_beta, w1, b1, out):
                     store(done[i - 2])
                 if 0 <= i < last:
                     leaky(i)
+                if i == 1:
+                    affine.append(scale_and_shift(1, by_pass))
                 if 0 < i <= last:
                     quantise(i - 1)
                     c, g = steps[i - 1]

@@ -58,7 +58,7 @@ def tile_roibaseline_pa_t_kernel(tc, h_enc, enc_gamma, enc_beta, w1, b1, out):
         junk_pool = ctx.enter_context(tc.tile_pool(name="junk", bufs=4))
         y_pool = ctx.enter_context(tc.tile_pool(name="y", bufs=4))
         c_pool = ctx.enter_context(tc.tile_pool(name="c", bufs=3))
-        q_pool = ctx.enter_context(tc.tile_pool(name="q", bufs=5))
+        q_pool = ctx.enter_context(tc.tile_pool(name="q", bufs=6))
         o_pool = ctx.enter_context(tc.tile_pool(name="o", bufs=3))
         xt_psum = [
             ctx.enter_context(tc.psum_pool(name="xt0", bufs=3)),
@@ -78,7 +78,7 @@ def tile_roibaseline_pa_t_kernel(tc, h_enc, enc_gamma, enc_beta, w1, b1, out):
         nc.vector.memset(minus_half[:], -0.5)
 
         w_rows = keep.tile([P, CHANNELS], BF16, name="w_rows")
-        nc.scalar.dma_start(out=w_rows[:], in_=w1)
+        nc.sync.dma_start(out=w_rows[:], in_=w1)
         x_chunks = []
         for c in range(CHUNKS):
             x_chunk = keep.tile([P, ROW_TILES, CHANNELS], BF16, name="x%d" % c)
@@ -93,6 +93,7 @@ def tile_roibaseline_pa_t_kernel(tc, h_enc, enc_gamma, enc_beta, w1, b1, out):
         gamma_bf = keep.tile([P, PASSES, 4], BF16, name="gamma_bf")
         beta_bf = keep.tile([P, PASSES, 4], BF16, name="beta_bf")
         bias_bf = keep.tile([P, 1], BF16, name="bias_bf")
+        bias_row = keep.tile([P, FEATURES], BF16, name="bias_row")
         nc.sync.dma_start(
             out=gamma_bf[:],
             in_=enc_gamma.rearrange("r o -> (r o)").rearrange("(g p t) -> p g t", g=PASSES, p=P),
@@ -102,6 +103,7 @@ def tile_roibaseline_pa_t_kernel(tc, h_enc, enc_gamma, enc_beta, w1, b1, out):
             in_=enc_beta.rearrange("r o -> (r o)").rearrange("(g p t) -> p g t", g=PASSES, p=P),
         )
         nc.sync.dma_start(out=bias_bf[:], in_=b1.rearrange("(f o) -> f o", o=1))
+        nc.sync.dma_start(out=bias_row[:], in_=b1.partition_broadcast(P))
 
         w_codes = keep.tile([P, PASSES * FEATURES], U32, name="w_codes", align_bytes=64)
         w_scales = keep.tile([P, PASSES * FEATURES], U8, name="w_scales", align_bytes=64)
@@ -136,7 +138,7 @@ def tile_roibaseline_pa_t_kernel(tc, h_enc, enc_gamma, enc_beta, w1, b1, out):
             nc.vector.memset(rows[:, u, :], float(banks * CHUNK))
         nc.vector.reciprocal(out=per_row[:], in_=rows[:])
 
-        def statistics(c, s):
+        def statistics(c, s, after=(None, None)):
             on_scalar = scalar_takes(c, s)
             bank = xt_psum[on_scalar].tile([P, CHUNK], F32, tag="xt", name="bank_a")
             transpose_words(nc, bank, x_chunks[c], s * P, 1, ident)
@@ -147,6 +149,8 @@ def tile_roibaseline_pa_t_kernel(tc, h_enc, enc_gamma, enc_beta, w1, b1, out):
                         in_=bank[:].bitcast(BF16)[:, h * BN_WIDTH : (h + 1) * BN_WIDTH],
                     )
                     bn_used[s] += 1
+                    if after[h]:
+                        after[h]()
                 return
             u = s - 2
             col = scalar_used[u]
@@ -154,6 +158,9 @@ def tile_roibaseline_pa_t_kernel(tc, h_enc, enc_gamma, enc_beta, w1, b1, out):
             sums.append((c, u, col))
             if c == 0:
                 nc.scalar.mul(out=neg_x0[:, u, :], in_=bank[:].bitcast(BF16)[:, 0:2], mul=-1.0)
+                nc.gpsimd.tensor_tensor(
+                    out=x0_sum[:, u, :], in0=neg_x0[:, u, :], in1=rows[:, u, :], op=ALU.mult
+                )
             for e in range(2):
                 junk = junk_pool.tile([P, CHUNK], BF16, name="junk")
                 nc.scalar.activation(
@@ -210,47 +217,28 @@ def tile_roibaseline_pa_t_kernel(tc, h_enc, enc_gamma, enc_beta, w1, b1, out):
             return by_pass
 
         def scale_and_shift(g, by_pass):
-            moments = keep.tile([P, 4, 2], F32, name="moments%d" % g)
-            nc.vector.tensor_copy(out=moments[:], in_=by_pass[:].rearrange("p u e m -> p (u e) m"))
+            moments = by_pass[:].rearrange("p u e m -> p (u e) m")
+            root = keep.tile([P, 4], F32, name="root%d" % g)
             scale = keep.tile([P, 4], F32, name="scale%d" % g)
             shift = keep.tile([P, 4], F32, name="shift%d" % g)
             cols = slice(4 * g, 4 * g + 4)
-            nc.gpsimd.tensor_scalar(
-                out=scale[:], in0=moments[:, :, 1], scalar1=EPS, scalar2=None, op0=ALU.add
-            )
-            nc.gpsimd.tensor_tensor(out=scale[:], in0=scale[:], in1=minus_half[:], op=ALU.pow)
-            nc.gpsimd.tensor_tensor(out=scale[:], in0=scale[:], in1=gamma[:, cols], op=ALU.mult)
-            nc.gpsimd.tensor_tensor(out=shift[:], in0=moments[:, :, 0], in1=scale[:], op=ALU.mult)
+            nc.vector.tensor_scalar_add(out=root[:], in0=moments[:, :, 1], scalar1=EPS)
+            nc.vector.tensor_mul(out=shift[:], in0=moments[:, :, 0], in1=gamma[:, cols])
+            nc.gpsimd.tensor_tensor(out=root[:], in0=root[:], in1=minus_half[:], op=ALU.pow)
+            nc.gpsimd.tensor_tensor(out=shift[:], in0=shift[:], in1=root[:], op=ALU.mult)
             nc.gpsimd.tensor_tensor(
                 out=shift[:], in0=beta[:, cols], in1=shift[:], op=ALU.subtract
             )
+            nc.gpsimd.tensor_tensor(out=scale[:], in0=root[:], in1=gamma[:, cols], op=ALU.mult)
             return scale, shift
 
-        engines = {mybir.EngineType.PE, mybir.EngineType.Activation, mybir.EngineType.DVE}
-        with tc.manual_schedule(engines=engines):
-            for c in range(CHUNKS):
-                for s in (0, 2, 1, 3):
-                    if (c, s) not in LATE_BANKS:
-                        statistics(c, s)
-                add_up()
-                if c == 1:
-                    prepare_w()
-            nc.gpsimd.tensor_copy(out=gamma[:], in_=gamma_bf[:].rearrange("p g t -> p (g t)"))
-            nc.gpsimd.tensor_copy(out=beta[:], in_=beta_bf[:].rearrange("p g t -> p (g t)"))
-            nc.gpsimd.tensor_copy(out=bias[:], in_=bias_bf[:])
-            mean_var = aggregate(0)
-            for bank in LATE_BANKS[:3]:
-                statistics(*bank)
-            by_pass = reorder(0, mean_var)
-            affine = [scale_and_shift(0, by_pass)]
-            for bank in LATE_BANKS[3:]:
-                statistics(*bank)
-            add_up()
+        x_sum = keep.tile([P, 2, 2], F32, name="x_sum")
+        sq_sum = keep.tile([P, 2, 2], F32, name="sq_sum")
+        x0_sum = keep.tile([P, 2, 2], F32, name="x0_sum")
+        off = keep.tile([P, 2, 2], F32, name="off")
+        share = bn_parts[:, 2:4, 0, :].rearrange("p u (e k) -> p u e k", k=3)
 
-            x_sum = keep.tile([P, 2, 2], F32, name="x_sum")
-            sq_sum = keep.tile([P, 2, 2], F32, name="sq_sum")
-            off = keep.tile([P, 2, 2], F32, name="off")
-            share = bn_parts[:, 2:4, 0, :].rearrange("p u (e k) -> p u e k", k=3)
+        def share_sums():
             for u in range(2):
                 used = scalar_used[u]
                 nc.vector.tensor_reduce(
@@ -259,22 +247,29 @@ def tile_roibaseline_pa_t_kernel(tc, h_enc, enc_gamma, enc_beta, w1, b1, out):
                 nc.vector.tensor_reduce(
                     out=sq_sum[:, u, :], in_=sq_parts[:, u, :, 0:used], axis=AXIS_X, op=ALU.add
                 )
+
+        def share_means():
+            nc.vector.tensor_add(out=off[:], in0=x_sum[:], in1=x0_sum[:])
             nc.vector.tensor_copy(out=share[:, :, :, 0], in_=rows[:])
             nc.vector.tensor_mul(out=share[:, :, :, 1], in0=x_sum[:], in1=per_row[:])
-            nc.vector.tensor_add(out=off[:], in0=share[:, :, :, 1], in1=neg_x0[:])
-            nc.vector.tensor_mul(out=off[:], in0=off[:], in1=off[:])
-            nc.vector.tensor_mul(out=off[:], in0=off[:], in1=rows[:])
-            nc.vector.tensor_sub(out=share[:, :, :, 2], in0=sq_sum[:], in1=off[:])
-            mean_var = aggregate(1)
 
-        steps = [(c, g) for g in range(PASSES) for c in range(4)]
-        steps += [(c, g) for c in range(4, CHUNKS) for g in range(PASSES)]
+        def share_offsets():
+            nc.vector.tensor_mul(out=off[:], in0=off[:], in1=off[:])
+
+        def share_variances():
+            for u in range(2):
+                nc.vector.scalar_tensor_tensor(
+                    out=share[:, u, :, 2],
+                    in0=off[:, u, :],
+                    scalar=-1.0 / (scalar_used[u] * CHUNK),
+                    in1=sq_sum[:, u, :],
+                    op0=ALU.mult,
+                    op1=ALU.add,
+                )
+
+        steps = [(c, g) for g in range(PASSES) for c in range(5)]
+        steps += [(c, g) for c in range(5, CHUNKS) for g in range(PASSES)]
         banks = {}
-        normed = {}
-        grouped = {}
-        chunk_codes = {}
-        by_feature = {}
-        turned = {}
 
         def turn(i):
             c, g = steps[i]
@@ -283,6 +278,36 @@ def tile_roibaseline_pa_t_kernel(tc, h_enc, enc_gamma, enc_beta, w1, b1, out):
                 bank = xt_psum[u].tile([P, CHUNK], F32, tag="xt", name="bank_b")
                 transpose_words(nc, bank, x_chunks[c], 256 * g + u, 2, ident)
                 banks[i].append(bank)
+
+        engines = {mybir.EngineType.PE, mybir.EngineType.Activation, mybir.EngineType.DVE}
+        with tc.manual_schedule(engines=engines):
+            prepare_w()
+            for c in range(CHUNKS):
+                for s in (0, 2, 1, 3):
+                    if (c, s) not in LATE_BANKS:
+                        statistics(c, s)
+                add_up()
+            nc.gpsimd.tensor_copy(out=gamma[:], in_=gamma_bf[:].rearrange("p g t -> p (g t)"))
+            nc.gpsimd.tensor_copy(out=beta[:], in_=beta_bf[:].rearrange("p g t -> p (g t)"))
+            nc.gpsimd.tensor_copy(out=bias[:], in_=bias_bf[:])
+            mean_var = aggregate(0)
+            for bank in LATE_BANKS[:3]:
+                statistics(*bank)
+            by_pass = reorder(0, mean_var)
+            affine = [scale_and_shift(0, by_pass)]
+            for bank in LATE_BANKS[3:6]:
+                statistics(*bank)
+            add_up()
+            turn(0)
+            statistics(*LATE_BANKS[6])
+            share_sums()
+            statistics(*LATE_BANKS[7], after=(share_means, share_offsets))
+
+        normed = {}
+        grouped = {}
+        chunk_codes = {}
+        by_feature = {}
+        turned = {}
 
         def norm(i, u):
             g = steps[i][1]
@@ -341,6 +366,34 @@ def tile_roibaseline_pa_t_kernel(tc, h_enc, enc_gamma, enc_beta, w1, b1, out):
                 )
             by_feature[c] = acc
 
+        def finish_last(c):
+            codes, scales = chunk_codes[c]
+            acc = acc_psum.tile([P, ROW_TILES, FEATURES], F32, tag="acc", name="acc_rows")
+            for j in range(ROW_TILES):
+                rows_j = slice(j * P, (j + 1) * P)
+                for g in range(PASSES):
+                    cols = slice(g * FEATURES, (g + 1) * FEATURES)
+                    nc.tensor.matmul_mx(
+                        out=acc[:, j, :],
+                        lhsT=codes[:, g, rows_j].bitcast(FP8X4),
+                        lhsT_scale=scales[:, g, rows_j],
+                        rhs=w_codes[:, cols].bitcast(FP8X4),
+                        rhs_scale=w_scales[:, cols],
+                        start=(g == 0),
+                        stop=(g == PASSES - 1),
+                    )
+            result = o_pool.tile([P, ROW_TILES, FEATURES], F32, name="result")
+            nc.vector.tensor_tensor(
+                out=result[:],
+                in0=acc[:],
+                in1=bias_row[:].unsqueeze(1).to_broadcast([P, ROW_TILES, FEATURES]),
+                op=ALU.add,
+            )
+            nc.sync.dma_start(
+                out=out[c * CHUNK : (c + 1) * CHUNK, :].rearrange("(p j) f -> p j f", j=ROW_TILES),
+                in_=result[:],
+            )
+
         def add_bias(c):
             biased = o_pool.tile([P, CHUNK], F32, name="biased")
             nc.scalar.activation(
@@ -364,10 +417,10 @@ def tile_roibaseline_pa_t_kernel(tc, h_enc, enc_gamma, enc_beta, w1, b1, out):
         last = len(steps)
         done = {}
         with tc.manual_schedule(engines=engines):
-            for i in range(-3, last + 3):
-                if i + 3 < last:
+            for i in range(-3, last + 1):
+                if 0 < i + 3 < last:
                     turn(i + 3)
-                if i == 0:
+                if i == 1:
                     by_pass = reorder(1, mean_var)
                 if 0 <= i + 2 < last:
                     norm(i + 2, 0)
@@ -378,11 +431,16 @@ def tile_roibaseline_pa_t_kernel(tc, h_enc, enc_gamma, enc_beta, w1, b1, out):
                     store(done[i - 2])
                 if 0 <= i < last:
                     leaky(i)
-                if i == 1:
+                if i == 0:
+                    share_variances()
+                    mean_var = aggregate(1)
+                if i == 2:
                     affine.append(scale_and_shift(1, by_pass))
                 if 0 < i <= last:
                     quantise(i - 1)
                     c, g = steps[i - 1]
-                    if g == PASSES - 1:
+                    if i == last:
+                        finish_last(c)
+                    elif g == PASSES - 1:
                         multiply(c)
                         done[i] = c

@@ -28,6 +28,7 @@ PASSES = 2
 BN_WIDTH = 512
 BN_CALLS = 2 * CHUNK // BN_WIDTH
 BN_SLOTS = CHUNKS * BN_CALLS
+EARLY_SLOTS = 3 * BN_SLOTS // 4
 
 LATE_BANKS = [(c, 2) for c in range(1, CHUNKS, 2)]
 
@@ -55,6 +56,7 @@ def tile_roibaseline_pa_t_kernel(tc, h_enc, enc_gamma, enc_beta, w1, b1, out):
     nc = tc.nc
     with ExitStack() as ctx:
         keep = ctx.enter_context(tc.tile_pool(name="keep", bufs=1))
+        merge_pool = ctx.enter_context(tc.tile_pool(name="merge", bufs=2))
         junk_pool = ctx.enter_context(tc.tile_pool(name="junk", bufs=4))
         y_pool = ctx.enter_context(tc.tile_pool(name="y", bufs=4))
         c_pool = ctx.enter_context(tc.tile_pool(name="c", bufs=3))
@@ -129,6 +131,43 @@ def tile_roibaseline_pa_t_kernel(tc, h_enc, enc_gamma, enc_beta, w1, b1, out):
         sq_parts = keep.tile([P, 2, 2, CHUNKS], F32, name="sq_parts")
         sum_parts = back_psum.tile([P, 2, 2, CHUNKS], F32, tag="back", name="sum_parts")
         bn_used = [1, 1, 1, 1]
+        wide_slots = keep.tile([P, 2, BN_SLOTS - 3 * EARLY_SLOTS // 4, 8], F32, name="wide_slots")
+        merged = wide_slots[:, :, :, 0:6]
+        half_merged = keep.tile([P, 2, EARLY_SLOTS // 2, 6], F32, name="half_merged")
+
+        def next_slot(s):
+            n = bn_used[s]
+            bn_used[s] += 1
+            if s < 2 and n > EARLY_SLOTS:
+                return merged[:, s, n - 1 - 3 * EARLY_SLOTS // 4, :]
+            return bn_parts[:, s, n, :]
+
+        def merge(out, parts, pairs, rows_each):
+            first = parts[:, :, 0 : 2 * pairs : 2, :].rearrange("p h n (e k) -> p h n e k", k=3)
+            second = parts[:, :, 1 : 2 * pairs : 2, :].rearrange("p h n (e k) -> p h n e k", k=3)
+            result = out.rearrange("p h n (e k) -> p h n e k", k=3)
+            for h in range(2):
+                m0, m1 = first[:, h, :, :, 1], second[:, h, :, :, 1]
+                v0, v1 = first[:, h, :, :, 2], second[:, h, :, :, 2]
+                count, mean, variance = [result[:, h, :, :, k] for k in range(3)]
+                apart = merge_pool.tile([P, pairs, 2], F32, name="apart")
+                nc.gpsimd.tensor_tensor(out=apart[:], in0=m0, in1=m1, op=ALU.subtract)
+                nc.gpsimd.tensor_tensor(out=apart[:], in0=apart[:], in1=apart[:], op=ALU.mult)
+                nc.gpsimd.tensor_scalar(
+                    out=apart[:],
+                    in0=apart[:],
+                    scalar1=rows_each / 2.0,
+                    scalar2=0.0,
+                    op0=ALU.mult,
+                    op1=ALU.add,
+                )
+                nc.gpsimd.tensor_tensor(out=variance, in0=v0, in1=v1, op=ALU.add)
+                nc.gpsimd.tensor_tensor(out=variance, in0=variance, in1=apart[:], op=ALU.add)
+                nc.gpsimd.tensor_tensor(out=mean, in0=m0, in1=m1, op=ALU.add)
+                nc.gpsimd.tensor_scalar(
+                    out=mean, in0=mean, scalar1=0.5, scalar2=0.0, op0=ALU.mult, op1=ALU.add
+                )
+                nc.gpsimd.memset(count, 2.0 * rows_each)
         sums = []
         scalar_used = [0, 0]
         rows = keep.tile([P, 2, 2], F32, name="rows")
@@ -145,10 +184,9 @@ def tile_roibaseline_pa_t_kernel(tc, h_enc, enc_gamma, enc_beta, w1, b1, out):
             if not on_scalar:
                 for h in range(BN_CALLS):
                     nc.vector.bn_stats(
-                        out=bn_parts[:, s, bn_used[s], :],
+                        out=next_slot(s),
                         in_=bank[:].bitcast(BF16)[:, h * BN_WIDTH : (h + 1) * BN_WIDTH],
                     )
-                    bn_used[s] += 1
                     if after[h]:
                         after[h]()
                 return
@@ -194,11 +232,10 @@ def tile_roibaseline_pa_t_kernel(tc, h_enc, enc_gamma, enc_beta, w1, b1, out):
             mean_var = keep.tile([P, 2, 2, 2], F32, name="mean_var%d" % g)
             for h in range(2):
                 s = 2 * g + h
-                first_slot = 0 if s >= 2 else 1
+                parts = merged[:, s] if g == 0 else bn_parts[:, s, 0 : bn_used[s]]
                 for e in range(2):
                     nc.vector.bn_aggr(
-                        out=mean_var[:, h, e, :],
-                        in_=bn_parts[:, s, first_slot : bn_used[s], 3 * e : 3 * e + 3],
+                        out=mean_var[:, h, e, :], in_=parts[:, :, 3 * e : 3 * e + 3]
                     )
             return mean_var
 
@@ -287,6 +324,15 @@ def tile_roibaseline_pa_t_kernel(tc, h_enc, enc_gamma, enc_beta, w1, b1, out):
                     if (c, s) not in LATE_BANKS:
                         statistics(c, s)
                 add_up()
+                if BN_CALLS * (c + 1) == EARLY_SLOTS:
+                    early = bn_parts[:, 0:2, 1 : 1 + EARLY_SLOTS, :]
+                    merge(half_merged[:], early, EARLY_SLOTS // 2, BN_WIDTH // 2)
+                    merge(
+                        merged[:, :, 0 : EARLY_SLOTS // 4, :],
+                        half_merged[:],
+                        EARLY_SLOTS // 4,
+                        BN_WIDTH,
+                    )
             nc.gpsimd.tensor_copy(out=gamma[:], in_=gamma_bf[:].rearrange("p g t -> p (g t)"))
             nc.gpsimd.tensor_copy(out=beta[:], in_=beta_bf[:].rearrange("p g t -> p (g t)"))
             nc.gpsimd.tensor_copy(out=bias[:], in_=bias_bf[:])
@@ -308,6 +354,7 @@ def tile_roibaseline_pa_t_kernel(tc, h_enc, enc_gamma, enc_beta, w1, b1, out):
         chunk_codes = {}
         by_feature = {}
         turned = {}
+        row_banks = []
 
         def norm(i, u):
             g = steps[i][1]
@@ -366,29 +413,30 @@ def tile_roibaseline_pa_t_kernel(tc, h_enc, enc_gamma, enc_beta, w1, b1, out):
                 )
             by_feature[c] = acc
 
-        def finish_last(c):
+        def multiply_last(c, g):
             codes, scales = chunk_codes[c]
-            acc = acc_psum.tile([P, ROW_TILES, FEATURES], F32, tag="acc", name="acc_rows")
+            cols = slice(g * FEATURES, (g + 1) * FEATURES)
             for j in range(ROW_TILES):
+                if g == 0:
+                    acc = xt_psum[j % 2].tile([P, FEATURES], F32, tag="xt", name="acc_rows")
+                    row_banks.append(acc)
                 rows_j = slice(j * P, (j + 1) * P)
-                for g in range(PASSES):
-                    cols = slice(g * FEATURES, (g + 1) * FEATURES)
-                    nc.tensor.matmul_mx(
-                        out=acc[:, j, :],
-                        lhsT=codes[:, g, rows_j].bitcast(FP8X4),
-                        lhsT_scale=scales[:, g, rows_j],
-                        rhs=w_codes[:, cols].bitcast(FP8X4),
-                        rhs_scale=w_scales[:, cols],
-                        start=(g == 0),
-                        stop=(g == PASSES - 1),
-                    )
+                nc.tensor.matmul_mx(
+                    out=row_banks[j][:],
+                    lhsT=codes[:, g, rows_j].bitcast(FP8X4),
+                    lhsT_scale=scales[:, g, rows_j],
+                    rhs=w_codes[:, cols].bitcast(FP8X4),
+                    rhs_scale=w_scales[:, cols],
+                    start=(g == 0),
+                    stop=(g == PASSES - 1),
+                )
+
+        def store_last(c):
             result = o_pool.tile([P, ROW_TILES, FEATURES], F32, name="result")
-            nc.vector.tensor_tensor(
-                out=result[:],
-                in0=acc[:],
-                in1=bias_row[:].unsqueeze(1).to_broadcast([P, ROW_TILES, FEATURES]),
-                op=ALU.add,
-            )
+            for j in range(ROW_TILES):
+                nc.vector.tensor_tensor(
+                    out=result[:, j, :], in0=row_banks[j][:], in1=bias_row[:], op=ALU.add
+                )
             nc.sync.dma_start(
                 out=out[c * CHUNK : (c + 1) * CHUNK, :].rearrange("(p j) f -> p j f", j=ROW_TILES),
                 in_=result[:],
@@ -439,8 +487,9 @@ def tile_roibaseline_pa_t_kernel(tc, h_enc, enc_gamma, enc_beta, w1, b1, out):
                 if 0 < i <= last:
                     quantise(i - 1)
                     c, g = steps[i - 1]
-                    if i == last:
-                        finish_last(c)
+                    if c == CHUNKS - 1:
+                        multiply_last(c, g)
                     elif g == PASSES - 1:
                         multiply(c)
                         done[i] = c
+            store_last(CHUNKS - 1)

from contextlib import ExitStack

import concourse.mybir as mybir
from concourse.masks import make_identity

F32 = mybir.dt.float32
BF16 = mybir.dt.bfloat16
U32 = mybir.dt.uint32
U8 = mybir.dt.uint8
FP8X4 = mybir.dt.float8_e4m3fn_x4
ALU = mybir.AluOpType
ACT = mybir.ActivationFunctionType
AXIS_X = mybir.AxisListType.X

P = 128
BATCH = 8192
CHANNELS = 1024
FEATURES = 128
EPS = 1e-5
SLOPE = 0.3

ROW_TILES = 4
CHUNK = P * ROW_TILES
CHUNKS = BATCH // CHUNK
WORDS = CHANNELS // 2
SLABS = WORDS // P
PASSES = 2
BN_WIDTH = 512
BN_CALLS = 2 * CHUNK // BN_WIDTH
BN_SLOTS = CHUNKS * BN_CALLS
EARLY_SLOTS = 3 * BN_SLOTS // 4

LATE_BANKS = [(c, 2) for c in range(1, CHUNKS, 2)]

FLOPS = 2 * BATCH * CHANNELS * FEATURES


def scalar_takes(c, s):
    return s >= 2 and ((c, s) not in LATE_BANKS or (c, s) in LATE_BANKS[2::3])


def transpose_words(nc, bank, x_chunk, first, step, ident):
    for j in range(ROW_TILES):
        nc.tensor.transpose(
            out=bank[:, j * P : (j + 1) * P],
            in_=x_chunk[:, j, :].bitcast(F32)[:, first : first + step * (P - 1) + 1 : step],
            identity=ident[:],
        )


def half(bank, e):
    return bank[:].bitcast(BF16).rearrange("p (b e) -> p b e", e=2)[:, :, e]


def tile_roibaseline_pa_t_kernel(tc, h_enc, enc_gamma, enc_beta, w1, b1, out):
    nc = tc.nc
    with ExitStack() as ctx:
        keep = ctx.enter_context(tc.tile_pool(name="keep", bufs=1))
        merge_pool = ctx.enter_context(tc.tile_pool(name="merge", bufs=2))
        junk_pool = ctx.enter_context(tc.tile_pool(name="junk", bufs=4))
        y_pool = ctx.enter_context(tc.tile_pool(name="y", bufs=4))
        c_pool = ctx.enter_context(tc.tile_pool(name="c", bufs=3))
        q_pool = ctx.enter_context(tc.tile_pool(name="q", bufs=6))
        o_pool = ctx.enter_context(tc.tile_pool(name="o", bufs=3))
        xt_psum = [
            ctx.enter_context(tc.psum_pool(name="xt0", bufs=3)),
            ctx.enter_context(tc.psum_pool(name="xt1", bufs=3)),
        ]
        acc_psum = ctx.enter_context(tc.psum_pool(name="acc", bufs=1))
        back_psum = ctx.enter_context(tc.psum_pool(name="back", bufs=1))

        ident = keep.tile([P, P], F32, name="ident")
        make_identity(nc, ident[:])
        ones = keep.tile([P, 1], BF16, name="ones")
        nc.vector.memset(ones[:], 1.0)
        wide_ident = keep.tile([P, 3 * P], F32, name="wide_ident")
        nc.gpsimd.memset(wide_ident[:], 0.0)
        nc.gpsimd.tensor_copy(out=wide_ident[:, P : 2 * P], in_=ident[:])
        minus_half = keep.tile([P, 4], F32, name="minus_half")
        nc.vector.memset(minus_half[:], -0.5)

        w_rows = keep.tile([P, CHANNELS], BF16, name="w_rows")
        nc.sync.dma_start(out=w_rows[:], in_=w1)
        x_chunks = []
        for c in range(CHUNKS):
            x_chunk = keep.tile([P, ROW_TILES, CHANNELS], BF16, name="x%d" % c)
            chunk_rows = h_enc[c * CHUNK : (c + 1) * CHUNK].rearrange(
                "(p j) r o -> p j (r o)", j=ROW_TILES
            )
            pieces = ROW_TILES if c == 0 else 1
            width = ROW_TILES // pieces
            for j in range(0, ROW_TILES, width):
                nc.sync.dma_start(out=x_chunk[:, j : j + width, :], in_=chunk_rows[:, j : j + width, :])
            x_chunks.append(x_chunk)
        gamma_bf = keep.tile([P, PASSES, 4], BF16, name="gamma_bf")
        beta_bf = keep.tile([P, PASSES, 4], BF16, name="beta_bf")
        bias_bf = keep.tile([P, 1], BF16, name="bias_bf")
        bias_row = keep.tile([P, FEATURES], BF16, name="bias_row")
        nc.sync.dma_start(
            out=gamma_bf[:],
            in_=enc_gamma.rearrange("r o -> (r o)").rearrange("(g p t) -> p g t", g=PASSES, p=P),
        )
        nc.sync.dma_start(
            out=beta_bf[:],
            in_=enc_beta.rearrange("r o -> (r o)").rearrange("(g p t) -> p g t", g=PASSES, p=P),
        )
        nc.sync.dma_start(out=bias_bf[:], in_=b1.rearrange("(f o) -> f o", o=1))
        nc.sync.dma_start(out=bias_row[:], in_=b1.partition_broadcast(P))

        w_codes = keep.tile([P, PASSES * FEATURES], U32, name="w_codes", align_bytes=64)
        w_scales = keep.tile([P, PASSES * FEATURES], U8, name="w_scales", align_bytes=64)

        def prepare_w():
            w_bank = acc_psum.tile([P, SLABS * P], F32, tag="acc", name="w_bank")
            for s in range(SLABS):
                first = 256 * (s // 2) + s % 2
                nc.tensor.transpose(
                    out=w_bank[:, s * P : (s + 1) * P],
                    in_=w_rows[:].bitcast(F32)[:, first : first + 2 * P - 1 : 2],
                    identity=ident[:],
                )
            w_grouped = keep.tile([P, PASSES * FEATURES * 4], BF16, name="w_grouped", align_bytes=64)
            nc.vector.tensor_copy(
                out=w_grouped[:].bitcast(F32).rearrange("p (g f u) -> p g f u", g=PASSES, u=2),
                in_=w_bank[:].rearrange("p (g u f) -> p g f u", g=PASSES, u=2),
            )
            nc.vector.quantize_mx(out=w_codes[:].bitcast(FP8X4), scales=w_scales[:], in_=w_grouped[:])

        bn_parts = keep.tile([P, SLABS, 1 + BN_SLOTS, 6], F32, name="bn_parts")
        neg_x0 = keep.tile([P, 2, 2], F32, name="neg_x0")
        sq_parts = keep.tile([P, 2, 2, CHUNKS], F32, name="sq_parts")
        sum_parts = back_psum.tile([P, 2, 2, CHUNKS], F32, tag="back", name="sum_parts")
        bn_used = [1, 1, 1, 1]
        wide_slots = keep.tile([P, 2, BN_SLOTS - 3 * EARLY_SLOTS // 4, 8], F32, name="wide_slots")
        merged = wide_slots[:, :, :, 0:6]
        half_merged = keep.tile([P, 2, EARLY_SLOTS // 2, 6], F32, name="half_merged")

        def next_slot(s):
            n = bn_used[s]
            bn_used[s] += 1
            if s < 2 and n > EARLY_SLOTS:
                return merged[:, s, n - 1 - 3 * EARLY_SLOTS // 4, :]
            return bn_parts[:, s, n, :]

        def merge(out, parts, pairs, rows_each):
            first = parts[:, :, 0 : 2 * pairs : 2, :].rearrange("p h n (e k) -> p h n e k", k=3)
            second = parts[:, :, 1 : 2 * pairs : 2, :].rearrange("p h n (e k) -> p h n e k", k=3)
            result = out.rearrange("p h n (e k) -> p h n e k", k=3)
            for h in range(2):
                m0, m1 = first[:, h, :, :, 1], second[:, h, :, :, 1]
                v0, v1 = first[:, h, :, :, 2], second[:, h, :, :, 2]
                count, mean, variance = [result[:, h, :, :, k] for k in range(3)]
                apart = merge_pool.tile([P, pairs, 2], F32, name="apart")
                nc.gpsimd.tensor_tensor(out=apart[:], in0=m0, in1=m1, op=ALU.subtract)
                nc.gpsimd.tensor_tensor(out=apart[:], in0=apart[:], in1=apart[:], op=ALU.mult)
                nc.gpsimd.tensor_scalar(
                    out=apart[:],
                    in0=apart[:],
                    scalar1=rows_each / 2.0,
                    scalar2=0.0,
                    op0=ALU.mult,
                    op1=ALU.add,
                )
                nc.gpsimd.tensor_tensor(out=variance, in0=v0, in1=v1, op=ALU.add)
                nc.gpsimd.tensor_tensor(out=variance, in0=variance, in1=apart[:], op=ALU.add)
                nc.gpsimd.tensor_tensor(out=mean, in0=m0, in1=m1, op=ALU.add)
                nc.gpsimd.tensor_scalar(
                    out=mean, in0=mean, scalar1=0.5, scalar2=0.0, op0=ALU.mult, op1=ALU.add
                )
                nc.gpsimd.memset(count, 2.0 * rows_each)
        sums = []
        scalar_used = [0, 0]
        rows = keep.tile([P, 2, 2], F32, name="rows")
        per_row = keep.tile([P, 2, 2], F32, name="per_row")
        for u in range(2):
            banks = sum(1 for c in range(CHUNKS) if scalar_takes(c, 2 + u))
            nc.vector.memset(rows[:, u, :], float(banks * CHUNK))
        nc.vector.reciprocal(out=per_row[:], in_=rows[:])

        def statistics(c, s, after=(None, None)):
            on_scalar = scalar_takes(c, s)
            bank = xt_psum[on_scalar].tile([P, CHUNK], F32, tag="xt", name="bank_a")
            transpose_words(nc, bank, x_chunks[c], s * P, 1, ident)
            if not on_scalar:
                for h in range(BN_CALLS):
                    nc.vector.bn_stats(
                        out=next_slot(s),
                        in_=bank[:].bitcast(BF16)[:, h * BN_WIDTH : (h + 1) * BN_WIDTH],
                    )
                    if after[h]:
                        after[h]()
                return
            u = s - 2
            col = scalar_used[u]
            scalar_used[u] += 1
            sums.append((c, u, col))
            if c == 0:
                nc.scalar.mul(out=neg_x0[:, u, :], in_=bank[:].bitcast(BF16)[:, 0:2], mul=-1.0)
                nc.gpsimd.tensor_tensor(
                    out=x0_sum[:, u, :], in0=neg_x0[:, u, :], in1=rows[:, u, :], op=ALU.mult
                )
            for e in range(2):
                junk = junk_pool.tile([P, CHUNK], BF16, name="junk")
                nc.scalar.activation(
                    out=junk[:],
                    in_=half(bank, e),
                    func=ACT.Square,
                    bias=neg_x0[:, u, e : e + 1],
                    scale=1.0,
                    accum_out=sq_parts[:, u, e, col : col + 1],
                )

        def add_up():
            for c, u, col in sums:
                for e in range(2):
                    first = 256 * (2 + u) + e
                    for j in range(ROW_TILES):
                        nc.tensor.matmul(
                            out=sum_parts[:, u, e, col : col + 1],
                            lhsT=x_chunks[c][:, j, first : first + 2 * P - 1 : 2],
                            rhs=ones[:],
                            start=(j == 0),
                            stop=(j == ROW_TILES - 1),
                        )
            sums.clear()

        gamma = keep.tile([P, SLABS * 2], F32, name="gamma")
        beta = keep.tile([P, SLABS * 2], F32, name="beta")
        bias = keep.tile([P, 1], F32, name="bias")

        def aggregate(g):
            mean_var = keep.tile([P, 2, 2, 2], F32, name="mean_var%d" % g)
            for h in range(2):
                s = 2 * g + h
                parts = merged[:, s] if g == 0 else bn_parts[:, s, 0 : bn_used[s]]
                for e in range(2):
                    nc.vector.bn_aggr(
                        out=mean_var[:, h, e, :], in_=parts[:, :, 3 * e : 3 * e + 3]
                    )
            return mean_var

        def reorder(g, mean_var):
            by_pass = acc_psum.tile([P, 2, 2, 2], F32, tag="acc", name="by_pass")
            for u in range(2):
                for h in range(2):
                    first = P + u - P * h
                    nc.tensor.matmul(
                        out=by_pass[:, u, :, :],
                        lhsT=wide_ident[:, first : first + 2 * P - 1 : 2],
                        rhs=mean_var[:, h, :, :],
                        start=(h == 0),
                        stop=(h == 1),
                    )
            return by_pass

        def scale_and_shift(g, by_pass):
            moments = by_pass[:].rearrange("p u e m -> p (u e) m")
            root = keep.tile([P, 4], F32, name="root%d" % g)
            scale = keep.tile([P, 4], F32, name="scale%d" % g)
            shift = keep.tile([P, 4], F32, name="shift%d" % g)
            cols = slice(4 * g, 4 * g + 4)
            nc.vector.tensor_scalar_add(out=root[:], in0=moments[:, :, 1], scalar1=EPS)
            nc.vector.tensor_mul(out=shift[:], in0=moments[:, :, 0], in1=gamma[:, cols])
            nc.gpsimd.tensor_tensor(out=root[:], in0=root[:], in1=minus_half[:], op=ALU.pow)
            nc.gpsimd.tensor_tensor(out=shift[:], in0=shift[:], in1=root[:], op=ALU.mult)
            nc.gpsimd.tensor_tensor(
                out=shift[:], in0=beta[:, cols], in1=shift[:], op=ALU.subtract
            )
            nc.gpsimd.tensor_tensor(out=scale[:], in0=root[:], in1=gamma[:, cols], op=ALU.mult)
            return scale, shift

        x_sum = keep.tile([P, 2, 2], F32, name="x_sum")
        sq_sum = keep.tile([P, 2, 2], F32, name="sq_sum")
        x0_sum = keep.tile([P, 2, 2], F32, name="x0_sum")
        off = keep.tile([P, 2, 2], F32, name="off")
        share = bn_parts[:, 2:4, 0, :].rearrange("p u (e k) -> p u e k", k=3)

        def share_sums():
            for u in range(2):
                used = scalar_used[u]
                nc.vector.tensor_reduce(
                    out=x_sum[:, u, :], in_=sum_parts[:, u, :, 0:used], axis=AXIS_X, op=ALU.add
                )
                nc.vector.tensor_reduce(
                    out=sq_sum[:, u, :], in_=sq_parts[:, u, :, 0:used], axis=AXIS_X, op=ALU.add
                )

        def share_means():
            nc.vector.tensor_add(out=off[:], in0=x_sum[:], in1=x0_sum[:])
            nc.vector.tensor_copy(out=share[:, :, :, 0], in_=rows[:])
            nc.vector.tensor_mul(out=share[:, :, :, 1], in0=x_sum[:], in1=per_row[:])

        def share_offsets():
            nc.vector.tensor_mul(out=off[:], in0=off[:], in1=off[:])

        def share_variances():
            for u in range(2):
                nc.vector.scalar_tensor_tensor(
                    out=share[:, u, :, 2],
                    in0=off[:, u, :],
                    scalar=-1.0 / (scalar_used[u] * CHUNK),
                    in1=sq_sum[:, u, :],
                    op0=ALU.mult,
                    op1=ALU.add,
                )

        steps = [(c, g) for g in range(PASSES) for c in range(5)]
        steps += [(c, g) for c in range(5, CHUNKS) for g in range(PASSES)]
        banks = {}

        def turn(i):
            c, g = steps[i]
            banks[i] = []
            for u in range(2):
                bank = xt_psum[u].tile([P, CHUNK], F32, tag="xt", name="bank_b")
                transpose_words(nc, bank, x_chunks[c], 256 * g + u, 2, ident)
                banks[i].append(bank)

        engines = {mybir.EngineType.PE, mybir.EngineType.Activation, mybir.EngineType.DVE}
        with tc.manual_schedule(engines=engines):
            prepare_w()
            for c in range(CHUNKS):
                for s in (0, 2, 1, 3):
                    if (c, s) not in LATE_BANKS:
                        statistics(c, s)
                add_up()
                if BN_CALLS * (c + 1) == EARLY_SLOTS:
                    early = bn_parts[:, 0:2, 1 : 1 + EARLY_SLOTS, :]
                    merge(half_merged[:], early, EARLY_SLOTS // 2, BN_WIDTH // 2)
                    merge(
                        merged[:, :, 0 : EARLY_SLOTS // 4, :],
                        half_merged[:],
                        EARLY_SLOTS // 4,
                        BN_WIDTH,
                    )
            nc.gpsimd.tensor_copy(out=gamma[:], in_=gamma_bf[:].rearrange("p g t -> p (g t)"))
            nc.gpsimd.tensor_copy(out=beta[:], in_=beta_bf[:].rearrange("p g t -> p (g t)"))
            nc.gpsimd.tensor_copy(out=bias[:], in_=bias_bf[:])
            mean_var = aggregate(0)
            for bank in LATE_BANKS[:3]:
                statistics(*bank)
            by_pass = reorder(0, mean_var)
            affine = [scale_and_shift(0, by_pass)]
            for bank in LATE_BANKS[3:6]:
                statistics(*bank)
            add_up()
            turn(0)
            statistics(*LATE_BANKS[6])
            share_sums()
            statistics(*LATE_BANKS[7], after=(share_means, share_offsets))

        normed = {}
        grouped = {}
        chunk_codes = {}
        by_feature = {}
        turned = {}
        row_banks = []

        def norm(i, u):
            g = steps[i][1]
            if u == 0:
                y = y_pool.tile([P, CHUNK // 4, 4, 4], F32, name="y")
                normed[i] = y
            for e in range(2):
                t = 2 * u + e
                nc.scalar.activation(
                    out=normed[i][:, :, t, :],
                    in_=half(banks[i][u], e).rearrange("p (i q) -> p q i", i=4),
                    func=ACT.Identity,
                    bias=affine[g][1][:, t : t + 1],
                    scale=affine[g][0][:, t : t + 1],
                )

        def leaky(i):
            woven = c_pool.tile([P, 4, CHUNK], BF16, name="woven", align_bytes=64)
            y_run = normed[i][:].rearrange("p q t i -> p (q t) i")
            nc.vector.scalar_tensor_tensor(
                out=woven[:].rearrange("p i k -> p k i"),
                in0=y_run,
                scalar=SLOPE,
                in1=y_run,
                op0=ALU.mult,
                op1=ALU.max,
            )
            grouped[i] = woven

        def quantise(i):
            c, g = steps[i]
            if g == 0:
                codes = q_pool.tile([P, PASSES, CHUNK], U32, name="codes", align_bytes=64)
                scales = q_pool.tile([P, PASSES, CHUNK], U8, name="scales", align_bytes=64)
                chunk_codes[c] = (codes, scales)
            codes, scales = chunk_codes[c]
            nc.vector.quantize_mx(
                out=codes[:, g, :].bitcast(FP8X4),
                scales=scales[:, g, :],
                in_=grouped[i][:].rearrange("p i k -> p (i k)"),
            )

        def multiply(c):
            codes, scales = chunk_codes[c]
            acc = acc_psum.tile([P, CHUNK], F32, tag="acc", name="acc")
            for g in range(PASSES):
                cols = slice(g * FEATURES, (g + 1) * FEATURES)
                nc.tensor.matmul_mx(
                    out=acc[:],
                    lhsT=w_codes[:, cols].bitcast(FP8X4),
                    lhsT_scale=w_scales[:, cols],
                    rhs=codes[:, g, :].bitcast(FP8X4),
                    rhs_scale=scales[:, g, :],
                    start=(g == 0),
                    stop=(g == PASSES - 1),
                )
            by_feature[c] = acc

        def multiply_last(c, g):
            codes, scales = chunk_codes[c]
            cols = slice(g * FEATURES, (g + 1) * FEATURES)
            for j in range(ROW_TILES):
                if g == 0:
                    acc = xt_psum[j % 2].tile([P, FEATURES], F32, tag="xt", name="acc_rows")
                    row_banks.append(acc)
                rows_j = slice(j * P, (j + 1) * P)
                nc.tensor.matmul_mx(
                    out=row_banks[j][:],
                    lhsT=codes[:, g, rows_j].bitcast(FP8X4),
                    lhsT_scale=scales[:, g, rows_j],
                    rhs=w_codes[:, cols].bitcast(FP8X4),
                    rhs_scale=w_scales[:, cols],
                    start=(g == 0),
                    stop=(g == PASSES - 1),
                )

        def store_last(c):
            result = o_pool.tile([P, ROW_TILES, FEATURES], F32, name="result")
            for j in range(ROW_TILES):
                nc.vector.tensor_tensor(
                    out=result[:, j, :], in0=row_banks[j][:], in1=bias_row[:], op=ALU.add
                )
            nc.sync.dma_start(
                out=out[c * CHUNK : (c + 1) * CHUNK, :].rearrange("(p j) f -> p j f", j=ROW_TILES),
                in_=result[:],
            )

        def add_bias(c):
            biased = o_pool.tile([P, CHUNK], F32, name="biased")
            nc.scalar.activation(
                out=biased[:], in_=by_feature[c][:], func=ACT.Identity, bias=bias[:], scale=1.0
            )
            back = back_psum.tile([P, ROW_TILES, FEATURES], F32, tag="back", name="back")
            for j in range(ROW_TILES):
                nc.tensor.transpose(
                    out=back[:, j, :], in_=biased[:, j * P : (j + 1) * P], identity=ident[:]
                )
            turned[c] = back

        def store(c):
            result = o_pool.tile([P, ROW_TILES, FEATURES], F32, name="result")
            nc.scalar.copy(out=result[:], in_=turned[c][:])
            nc.sync.dma_start(
                out=out[c * CHUNK : (c + 1) * CHUNK, :].rearrange("(p j) f -> p j f", j=ROW_TILES),
                in_=result[:],
            )

        last = len(steps)
        done = {}
        with tc.manual_schedule(engines=engines):
            for i in range(-3, last + 1):
                if 0 < i + 3 < last:
                    turn(i + 3)
                if i == 1:
                    by_pass = reorder(1, mean_var)
                if 0 <= i + 2 < last:
                    norm(i + 2, 0)
                    norm(i + 2, 1)
                if i - 1 in done:
                    add_bias(done[i - 1])
                if i - 2 in done:
                    store(done[i - 2])
                if 0 <= i < last:
                    leaky(i)
                if i == 0:
                    share_variances()
                    mean_var = aggregate(1)
                if i == 2:
                    affine.append(scale_and_shift(1, by_pass))
                if 0 < i <= last:
                    quantise(i - 1)
                    c, g = steps[i - 1]
                    if c == CHUNKS - 1:
                        multiply_last(c, g)
                    elif g == PASSES - 1:
                        multiply(c)
                        done[i] = c
            store_last(CHUNKS - 1)
